import numpy as np
import ml_dtypes


def mxq(x, axis, fmt="e4m3"):
    dtype, down = {"e4m3": (ml_dtypes.float8_e4m3fn, 7), "e5m2": (ml_dtypes.float8_e5m2, 14)}[fmt]
    v = np.moveaxis(np.asarray(x, np.float32).astype(ml_dtypes.bfloat16).astype(np.float64), axis, -1)
    blocks = v.reshape(v.shape[:-1] + (-1, 32))
    amax = np.abs(blocks).max(-1, keepdims=True)
    byte = np.maximum(np.where(amax > 0, np.frexp(amax)[1] - 1 + 127, 0) - down, 1)
    scale = np.exp2(byte - 127.0)
    codes = (blocks / scale).astype(np.float32).astype(dtype).astype(np.float64)
    return np.moveaxis((codes * scale).reshape(v.shape), -1, axis)


WIDE = False


def mx_kscale(k):
    if not WIDE:
        return np.ones(k)
    levels = np.array([10, -10, 5, -5, 0])
    a = np.random.permutation(np.resize(levels, k // 512 * 4)).reshape(k // 512, 4)
    idx = np.arange(k)
    return np.exp2(a[idx // 512, idx % 128 // 32])


BF16 = ml_dtypes.bfloat16


def bf(x):
    return np.asarray(x, np.float32).astype(BF16)


def f64(x):
    return np.asarray(x).astype(np.float64)


B, S, D, W = 1, 4096, 256, 256
NB = S // W
NEG = -10000.0
SCALE = 1.0 / np.sqrt(D)
QC = 0.75


def setup_inputs():
    x = np.random.standard_normal((B, S, 3 * D))
    x[..., :2 * D] *= 1.4
    t = np.tile(np.sort(mx_kscale(2 * W))[::2], NB)
    x[..., 0] = QC * np.sqrt(D)
    x[..., D] -= np.log(t) / QC
    x[..., 2 * D:] *= (t / t.min())[:, None]
    return {"qkv": bf(x)}


def reference(qkv):
    x = f64(qkv)
    q, k, v = x[..., :D], x[..., D:2 * D], x[..., 2 * D:]
    win = (np.maximum(np.arange(NB) - 1, 0) * W)[:, None] + np.arange(2 * W)[None, :]
    i = np.arange(S).reshape(NB, W, 1)
    j = win[:, None, :]
    mask = np.where((j <= i) & (j >= i - W), 0.0, NEG)
    s = q.reshape(B, NB, W, D) @ k[:, win].transpose(0, 1, 3, 2) * SCALE + mask
    e = np.exp(s - s.max(-1, keepdims=True))
    vq = mxq(v, 1, "e4m3")
    o = (mxq(e, 3, "e4m3") @ vq[:, win]) / e.sum(-1, keepdims=True)
    return o.reshape(B, S, D)

@@ -1,0 +1,287 @@
+from contextlib import ExitStack
+
+import concourse.mybir as mybir
+from concourse.masks import make_identity
+
+F32 = mybir.dt.float32
+BF16 = mybir.dt.bfloat16
+U32 = mybir.dt.uint32
+U8 = mybir.dt.uint8
+FP8X4 = mybir.dt.float8_e4m3fn_x4
+ACT = mybir.ActivationFunctionType
+ALU = mybir.AluOpType
+AXIS = mybir.AxisListType
+
+P = 128
+PACK = 4
+SEQ = 4096
+D = 256
+PAIRS = D // 2
+BLOCK = 256
+HALVES = BLOCK // P
+N_BLOCKS = SEQ // BLOCK
+WINDOW = 2 * BLOCK
+CHUNK = 128
+QUARTER = CHUNK // PACK
+N_CHUNKS = SEQ // CHUNK
+ROWS = P * PACK
+N_LOADS = SEQ // ROWS
+SLOTS = 3
+SCALE = 1.0 / 16.0
+HIDDEN = -10000.0 / SCALE
+E_RING = 3
+AHEAD = 3
+
+FLOPS = 2 * (2 * SEQ * WINDOW * D)
+
+
+def tile_slidingselfattention_pa_t_kernel(tc, qkv, out):
+    nc = tc.nc
+    with ExitStack() as ctx:
+        keep = ctx.enter_context(tc.tile_pool(name="keep", bufs=1))
+        work = ctx.enter_context(tc.tile_pool(name="work", bufs=3))
+        small = ctx.enter_context(tc.tile_pool(name="small", bufs=6))
+        psum_s = ctx.enter_context(tc.psum_pool(name="psum_s", bufs=4))
+        psum_x = ctx.enter_context(tc.psum_pool(name="psum_x", bufs=1))
+        psum_t = ctx.enter_context(tc.psum_pool(name="psum_t", bufs=2))
+        psum_o = ctx.enter_context(tc.psum_pool(name="psum_o", bufs=1))
+
+        raw = []
+        shifted_v = {}
+        for g in range(N_LOADS):
+            raw_g = keep.tile([P, PACK, 3 * D], BF16, name="raw%d" % g)
+            nc.sync.dma_start(
+                out=raw_g[:],
+                in_=qkv[0, g * ROWS : (g + 1) * ROWS, :].rearrange("(p j) c -> p j c", j=PACK),
+            )
+            raw.append(raw_g)
+            if g + 1 < N_LOADS:
+                first_key = g * ROWS + BLOCK
+                v_again = keep.tile([P, PACK, D], BF16, name="shifted_v%d" % g)
+                nc.sync.dma_start(
+                    out=v_again[:],
+                    in_=qkv[0, first_key : first_key + WINDOW, 2 * D : 3 * D].rearrange(
+                        "(p j) c -> p j c", j=PACK
+                    ),
+                )
+                shifted_v[2 * g + 2] = v_again
+
+        ident_f32 = keep.tile([P, P], F32, name="ident_f32")
+        make_identity(nc, ident_f32[:])
+        ident_bf16 = keep.tile([P, P], BF16, name="ident_bf16")
+        make_identity(nc, ident_bf16[:])
+        mask_rows = keep.tile([P, 2, CHUNK], F32, name="mask_rows")
+        nc.gpsimd.memset(mask_rows[:], 0.0)
+        nc.gpsimd.affine_select(
+            out=mask_rows[:, 0, :], in_=mask_rows[:, 0, :], compare_op=ALU.is_ge, fill=HIDDEN,
+            base=0, pattern=[[1, CHUNK]], channel_multiplier=-1,
+        )
+        nc.gpsimd.affine_select(
+            out=mask_rows[:, 1, :], in_=mask_rows[:, 1, :], compare_op=ALU.is_ge, fill=HIDDEN,
+            base=0, pattern=[[-1, CHUNK]], channel_multiplier=1,
+        )
+        mask = keep.tile([P, 2, CHUNK], BF16, name="mask")
+        nc.vector.tensor_copy(
+            out=mask[:].rearrange("i m (t r) -> i m t r", t=PACK),
+            in_=mask_rows[:].rearrange("i m (r t) -> i m t r", t=PACK),
+        )
+
+        e_first = [keep.tile([P, PACK, P], BF16, name="e_first%d" % h) for h in range(HALVES)]
+        e_ring = [
+            [keep.tile([P, PACK, P], BF16, name="e_ring%d_%d" % (h, i)) for i in range(E_RING)]
+            for h in range(HALVES)
+        ]
+        for h in range(HALVES):
+            for e_tile in [e_first[h]] + e_ring[h]:
+                nc.vector.memset(e_tile[:], 0.0)
+
+        q_t = keep.tile([P, SEQ], F32, name="q_t")
+        k_t = keep.tile([P, SEQ], F32, name="k_t")
+        q_t_bf16 = q_t[:].bitcast(BF16).rearrange("w (i f) -> w i f", f=2)
+        k_t_bf16 = k_t[:].bitcast(BF16).rearrange("w (c x f) -> w c x f", c=N_CHUNKS, f=2)
+
+        v_codes = keep.tile([P, N_BLOCKS, D], U32, name="v_codes", align_bytes=64)
+        v_scales = keep.tile([P, N_BLOCKS, D], U8, name="v_scales", align_bytes=64)
+
+        def transpose_rows(g, first_word, is_key):
+            words = raw[g][:].bitcast(F32)
+            flipped = psum_x.tile([P, PACK, P], F32, tag="flipped")
+            for j in range(PACK):
+                nc.tensor.transpose(
+                    flipped[:, j, :], words[:, j, first_word : first_word + PAIRS], ident_f32[:]
+                )
+            columns = slice(g * ROWS, (g + 1) * ROWS)
+            if is_key:
+                nc.vector.tensor_copy(
+                    out=k_t[:, columns].rearrange("w (c t r) -> w c t r", t=PACK, r=QUARTER),
+                    in_=flipped[:].rearrange("w t (c r) -> w c t r", r=QUARTER),
+                )
+            else:
+                nc.vector.tensor_copy(
+                    out=q_t[:, columns].rearrange("w (p j) -> w p j", j=PACK),
+                    in_=flipped[:].rearrange("w j p -> w p j"),
+                )
+
+        def transpose_next(item):
+            if item < 2 * N_LOADS:
+                transpose_rows(item // 2, (item % 2) * PAIRS, item % 2 == 1)
+
+        grouped_v = {}
+
+        def group_v(n):
+            rows = shifted_v[n][:] if n in shifted_v else raw[n // 2][:, :, 2 * D : 3 * D]
+            grouped_v[n] = work.tile([P, D, PACK], BF16, name="grouped_v", align_bytes=64)
+            nc.vector.tensor_copy(
+                out=grouped_v[n][:].rearrange("p (c i) t -> p c t i", i=4),
+                in_=rows.rearrange("p t (c i) -> p c t i", i=4),
+            )
+
+        def quantise_v(n):
+            nc.vector.quantize_mx(
+                out=v_codes[:, n, :].bitcast(FP8X4),
+                scales=v_scales[:, n, :],
+                in_=grouped_v[n][:].rearrange("p d t -> p (d t)"),
+            )
+
+        scores = {}
+        shifts = {}
+        row_sums = {}
+        e_tiles = {}
+        flipped_e = {}
+        grouped_e = {}
+        e_codes = {}
+        e_scales = {}
+        summed = {}
+
+        def first_slot(u):
+            return max(0, SLOTS - 1 - u)
+
+        def score(n, h):
+            u = HALVES * n + h
+            s = psum_s.tile([P, SLOTS, CHUNK], F32, name="s")
+            q_half = q_t_bf16[:, u * P : (u + 1) * P, :]
+            if u >= 1:
+                for f in range(2):
+                    nc.tensor.matmul(
+                        out=s[:, 1, :], lhsT=q_half[:, :, f], rhs=k_t_bf16[:, u - 1, :, f],
+                        start=(f == 0), stop=(f == 1),
+                    )
+            if u >= 2:
+                edge_slots, edge_chunks, edge_masks = slice(0, 3, 2), slice(u - 2, u + 1, 2), slice(0, 2)
+            else:
+                edge_slots, edge_chunks, edge_masks = slice(2, 3), slice(u, u + 1), slice(1, 2)
+            nc.tensor.matmul(
+                out=s[:, edge_slots, :], lhsT=ident_bf16[:], rhs=mask[:, edge_masks, :],
+                start=True, stop=False,
+            )
+            for f in range(2):
+                nc.tensor.matmul(
+                    out=s[:, edge_slots, :], lhsT=q_half[:, :, f], rhs=k_t_bf16[:, edge_chunks, :, f],
+                    start=False, stop=(f == 1),
+                )
+            row_max = small.tile([P, 1], F32, name="row_max")
+            nc.vector.reduce_max(out=row_max[:], in_=s[:, first_slot(u) : SLOTS, :], axis=AXIS.XY)
+            shift = small.tile([P, 1], F32, name="shift")
+            nc.vector.tensor_scalar(
+                out=shift[:], in0=row_max[:], scalar1=-SCALE, scalar2=None, op0=ALU.mult
+            )
+            scores[n, h] = s
+            shifts[n, h] = shift
+
+        def exponentials(n):
+            e_tiles[n] = e_first if n == 0 else [e_ring[h][n % E_RING] for h in range(HALVES)]
+            row_sums[n] = small.tile([P, HALVES], F32, name="row_sums")
+            for h in range(HALVES):
+                u = HALVES * n + h
+                first = first_slot(u)
+                seen = SLOTS - first
+                quarter = u - 2 + first - HALVES * max(n - 1, 0)
+                nc.scalar.activation(
+                    out=e_tiles[n][h][:, :, quarter * QUARTER : (quarter + seen) * QUARTER].rearrange(
+                        "i t (k r) -> i t k r", r=QUARTER
+                    ),
+                    in_=scores[n, h][:, first:SLOTS, :].rearrange("i k (t r) -> i t k r", t=PACK),
+                    func=ACT.Exp, bias=shifts[n, h][:], scale=SCALE,
+                    accum_out=row_sums[n][:, h : h + 1],
+                )
+
+        def transpose_e(n):
+            flipped_e[n] = psum_t.tile([P, HALVES, PACK, P], BF16, name="flipped_e")
+            for h in range(HALVES):
+                for t in range(PACK):
+                    nc.tensor.transpose(flipped_e[n][:, h, t, :], e_tiles[n][h][:, t, :], ident_bf16[:])
+
+        def group_e(n):
+            grouped_e[n] = work.tile([P, HALVES, P, PACK], BF16, name="grouped_e", align_bytes=64)
+            nc.scalar.copy(out=grouped_e[n][:], in_=flipped_e[n][:].rearrange("p h t i -> p h i t"))
+
+        def quantise_e(n):
+            e_codes[n] = work.tile([P, HALVES * P], U32, name="e_codes", align_bytes=64)
+            e_scales[n] = work.tile([P, HALVES * P], U8, name="e_scales", align_bytes=64)
+            nc.vector.quantize_mx(
+                out=e_codes[n][:].bitcast(FP8X4),
+                scales=e_scales[n][:],
+                in_=grouped_e[n][:].rearrange("p h i t -> p (h i t)"),
+            )
+
+        def weighted_sum(n):
+            window = max(n, 1)
+            summed[n] = psum_o.tile([P, HALVES, D], F32, name="summed")
+            for h in range(HALVES):
+                nc.tensor.matmul_mx(
+                    out=summed[n][:, h, :],
+                    lhsT=e_codes[n][:, h * P : (h + 1) * P].bitcast(FP8X4),
+                    lhsT_scale=e_scales[n][:, h * P : (h + 1) * P],
+                    rhs=v_codes[:, window, :].bitcast(FP8X4),
+                    rhs_scale=v_scales[:, window, :],
+                    start=True, stop=True,
+                )
+
+        inverse = {}
+
+        def invert_row_sums(n):
+            inverse[n] = small.tile([P, HALVES], F32, name="inverse")
+            nc.vector.reciprocal(out=inverse[n][:], in_=row_sums[n][:])
+
+        def divide_and_store(n):
+            result = work.tile([P, HALVES, D], F32, name="result")
+            for h in range(HALVES):
+                nc.scalar.activation(
+                    out=result[:, h, :], in_=summed[n][:, h, :], func=ACT.Copy,
+                    scale=inverse[n][:, h : h + 1],
+                )
+            nc.sync.dma_start(
+                out=out[0, n * BLOCK : (n + 1) * BLOCK, :].rearrange("(h p) d -> p h d", h=HALVES),
+                in_=result[:],
+            )
+
+        def is_block(n):
+            return 0 <= n < N_BLOCKS
+
+        with tc.manual_schedule():
+            for item in range(AHEAD):
+                transpose_next(item)
+            for k in range(N_BLOCKS + 3):
+                if is_block(k - 2):
+                    group_e(k - 2)
+                if is_block(k):
+                    score(k, 0)
+                if is_block(k - 2):
+                    quantise_e(k - 2)
+                if is_block(k - 3):
+                    invert_row_sums(k - 3)
+                if is_block(k):
+                    score(k, 1)
+                if is_block(k - 3):
+                    divide_and_store(k - 3)
+                if is_block(k):
+                    exponentials(k)
+                transpose_next(k + AHEAD)
+                if 1 <= k < N_BLOCKS:
+                    quantise_v(k)
+                if 1 <= k + 1 < N_BLOCKS:
+                    group_v(k + 1)
+                if is_block(k - 1):
+                    transpose_e(k - 1)
+                if is_block(k - 2):
+                    weighted_sum(k - 2)

@@ -23,9 +23,9 @@ N_BLOCKS = SEQ // BLOCK
 WINDOW = 2 * BLOCK
 CHUNK = 128
 QUARTER = CHUNK // PACK
-N_CHUNKS = SEQ // CHUNK
 ROWS = P * PACK
 N_LOADS = SEQ // ROWS
+LOAD_CHUNKS = ROWS // CHUNK
 SLOTS = 3
 SCALE = 1.0 / 16.0
 HIDDEN = -10000.0 / SCALE
@@ -95,13 +95,19 @@ def tile_slidingselfattention_pa_t_kernel(tc, qkv, out):
             for e_tile in [e_first[h]] + e_ring[h]:
                 nc.vector.memset(e_tile[:], 0.0)
 
-        q_t = keep.tile([P, SEQ], F32, name="q_t")
-        k_t = keep.tile([P, SEQ], F32, name="k_t")
-        q_t_bf16 = q_t[:].bitcast(BF16).rearrange("w (i f) -> w i f", f=2)
-        k_t_bf16 = k_t[:].bitcast(BF16).rearrange("w (c x f) -> w c x f", c=N_CHUNKS, f=2)
+        q_t = [keep.tile([P, ROWS], F32, name="q_t%d" % g) for g in range(N_LOADS)]
+        k_t = [keep.tile([P, ROWS], F32, name="k_t%d" % g) for g in range(N_LOADS)]
 
-        v_codes = keep.tile([P, N_BLOCKS, D], U32, name="v_codes", align_bytes=64)
-        v_scales = keep.tile([P, N_BLOCKS, D], U8, name="v_scales", align_bytes=64)
+        def q_columns(u, f):
+            halves = q_t[u // LOAD_CHUNKS][:].bitcast(BF16).rearrange("w (c i f) -> w c i f", c=LOAD_CHUNKS, f=2)
+            return halves[:, u % LOAD_CHUNKS, :, f]
+
+        def k_columns(c, f):
+            chunks = k_t[c // LOAD_CHUNKS][:].bitcast(BF16).rearrange("w (c x f) -> w c x f", c=LOAD_CHUNKS, f=2)
+            return chunks[:, c % LOAD_CHUNKS, :, f]
+
+        v_codes = {}
+        v_scales = {}
 
         def transpose_rows(g, first_word, is_key):
             words = raw[g][:].bitcast(F32)
@@ -110,15 +116,14 @@ def tile_slidingselfattention_pa_t_kernel(tc, qkv, out):
                 nc.tensor.transpose(
                     flipped[:, j, :], words[:, j, first_word : first_word + PAIRS], ident_f32[:]
                 )
-            columns = slice(g * ROWS, (g + 1) * ROWS)
             if is_key:
                 nc.vector.tensor_copy(
-                    out=k_t[:, columns].rearrange("w (c t r) -> w c t r", t=PACK, r=QUARTER),
+                    out=k_t[g][:].rearrange("w (c t r) -> w c t r", t=PACK, r=QUARTER),
                     in_=flipped[:].rearrange("w t (c r) -> w c t r", r=QUARTER),
                 )
             else:
                 nc.vector.tensor_copy(
-                    out=q_t[:, columns].rearrange("w (p j) -> w p j", j=PACK),
+                    out=q_t[g][:].rearrange("w (p j) -> w p j", j=PACK),
                     in_=flipped[:].rearrange("w j p -> w p j"),
                 )
 
@@ -137,13 +142,16 @@ def tile_slidingselfattention_pa_t_kernel(tc, qkv, out):
             )
 
         def quantise_v(n):
+            v_codes[n] = keep.tile([P, D], U32, name="v_codes%d" % n, align_bytes=64)
+            v_scales[n] = keep.tile([P, D], U8, name="v_scales%d" % n, align_bytes=64)
             nc.vector.quantize_mx(
-                out=v_codes[:, n, :].bitcast(FP8X4),
-                scales=v_scales[:, n, :],
+                out=v_codes[n][:].bitcast(FP8X4),
+                scales=v_scales[n][:],
                 in_=grouped_v[n][:].rearrange("p d t -> p (d t)"),
             )
 
         scores = {}
+        row_max = {}
         shifts = {}
         row_sums = {}
         e_tiles = {}
@@ -159,34 +167,29 @@ def tile_slidingselfattention_pa_t_kernel(tc, qkv, out):
         def score(n, h):
             u = HALVES * n + h
             s = psum_s.tile([P, SLOTS, CHUNK], F32, name="s")
-            q_half = q_t_bf16[:, u * P : (u + 1) * P, :]
-            if u >= 1:
+            for slot in range(first_slot(u), SLOTS):
+                if slot != 1:
+                    nc.tensor.matmul(
+                        out=s[:, slot, :], lhsT=ident_bf16[:], rhs=mask[:, slot // 2, :],
+                        start=True, stop=False,
+                    )
                 for f in range(2):
                     nc.tensor.matmul(
-                        out=s[:, 1, :], lhsT=q_half[:, :, f], rhs=k_t_bf16[:, u - 1, :, f],
-                        start=(f == 0), stop=(f == 1),
+                        out=s[:, slot, :], lhsT=q_columns(u, f), rhs=k_columns(u - 2 + slot, f),
+                        start=(slot == 1 and f == 0), stop=(f == 1),
                     )
-            if u >= 2:
-                edge_slots, edge_chunks, edge_masks = slice(0, 3, 2), slice(u - 2, u + 1, 2), slice(0, 2)
-            else:
-                edge_slots, edge_chunks, edge_masks = slice(2, 3), slice(u, u + 1), slice(1, 2)
-            nc.tensor.matmul(
-                out=s[:, edge_slots, :], lhsT=ident_bf16[:], rhs=mask[:, edge_masks, :],
-                start=True, stop=False,
-            )
-            for f in range(2):
-                nc.tensor.matmul(
-                    out=s[:, edge_slots, :], lhsT=q_half[:, :, f], rhs=k_t_bf16[:, edge_chunks, :, f],
-                    start=False, stop=(f == 1),
-                )
-            row_max = small.tile([P, 1], F32, name="row_max")
-            nc.vector.reduce_max(out=row_max[:], in_=s[:, first_slot(u) : SLOTS, :], axis=AXIS.XY)
-            shift = small.tile([P, 1], F32, name="shift")
-            nc.vector.tensor_scalar(
-                out=shift[:], in0=row_max[:], scalar1=-SCALE, scalar2=None, op0=ALU.mult
+            if h == 0:
+                row_max[n] = small.tile([P, HALVES], F32, name="row_max")
+            nc.vector.reduce_max(
+                out=row_max[n][:, h : h + 1], in_=s[:, first_slot(u) : SLOTS, :], axis=AXIS.XY
             )
             scores[n, h] = s
-            shifts[n, h] = shift
+
+        def scale_row_max(n):
+            shifts[n] = small.tile([P, HALVES], F32, name="shift")
+            nc.vector.tensor_scalar(
+                out=shifts[n][:], in0=row_max[n][:], scalar1=-SCALE, scalar2=None, op0=ALU.mult
+            )
 
         def exponentials(n):
             e_tiles[n] = e_first if n == 0 else [e_ring[h][n % E_RING] for h in range(HALVES)]
@@ -201,7 +204,7 @@ def tile_slidingselfattention_pa_t_kernel(tc, qkv, out):
                         "i t (k r) -> i t k r", r=QUARTER
                     ),
                     in_=scores[n, h][:, first:SLOTS, :].rearrange("i k (t r) -> i t k r", t=PACK),
-                    func=ACT.Exp, bias=shifts[n, h][:], scale=SCALE,
+                    func=ACT.Exp, bias=shifts[n][:, h : h + 1], scale=SCALE,
                     accum_out=row_sums[n][:, h : h + 1],
                 )
 
@@ -232,8 +235,8 @@ def tile_slidingselfattention_pa_t_kernel(tc, qkv, out):
                     out=summed[n][:, h, :],
                     lhsT=e_codes[n][:, h * P : (h + 1) * P].bitcast(FP8X4),
                     lhsT_scale=e_scales[n][:, h * P : (h + 1) * P],
-                    rhs=v_codes[:, window, :].bitcast(FP8X4),
-                    rhs_scale=v_scales[:, window, :],
+                    rhs=v_codes[window][:].bitcast(FP8X4),
+                    rhs_scale=v_scales[window][:],
                     start=True, stop=True,
                 )
 
@@ -259,29 +262,32 @@ def tile_slidingselfattention_pa_t_kernel(tc, qkv, out):
             return 0 <= n < N_BLOCKS
 
         with tc.manual_schedule():
-            for item in range(AHEAD):
-                transpose_next(item)
+            transpose_next(0)
+            transpose_next(1)
+            next_item = 2
             for k in range(N_BLOCKS + 3):
                 if is_block(k - 2):
                     group_e(k - 2)
                 if is_block(k):
                     score(k, 0)
+                    score(k, 1)
                 if is_block(k - 2):
                     quantise_e(k - 2)
-                if is_block(k - 3):
-                    invert_row_sums(k - 3)
                 if is_block(k):
-                    score(k, 1)
+                    scale_row_max(k)
+                if is_block(k - 1):
+                    invert_row_sums(k - 1)
                 if is_block(k - 3):
+                    weighted_sum(k - 3)
                     divide_and_store(k - 3)
                 if is_block(k):
                     exponentials(k)
-                transpose_next(k + AHEAD)
                 if 1 <= k < N_BLOCKS:
                     quantise_v(k)
+                while next_item <= k + AHEAD:
+                    transpose_next(next_item)
+                    next_item += 1
                 if 1 <= k + 1 < N_BLOCKS:
                     group_v(k + 1)
                 if is_block(k - 1):
                     transpose_e(k - 1)
-                if is_block(k - 2):
-                    weighted_sum(k - 2)

@@ -30,7 +30,6 @@ SLOTS = 3
 SCALE = 1.0 / 16.0
 HIDDEN = -10000.0 / SCALE
 E_RING = 3
-AHEAD = 3
 
 FLOPS = 2 * (2 * SEQ * WINDOW * D)
 
@@ -55,8 +54,8 @@ def tile_slidingselfattention_pa_t_kernel(tc, qkv, out):
                 in_=qkv[0, g * ROWS : (g + 1) * ROWS, :].rearrange("(p j) c -> p j c", j=PACK),
             )
             raw.append(raw_g)
-            if g + 1 < N_LOADS:
-                first_key = g * ROWS + BLOCK
+            if g >= 1:
+                first_key = g * ROWS - BLOCK
                 v_again = keep.tile([P, PACK, D], BF16, name="shifted_v%d" % g)
                 nc.sync.dma_start(
                     out=v_again[:],
@@ -64,7 +63,7 @@ def tile_slidingselfattention_pa_t_kernel(tc, qkv, out):
                         "(p j) c -> p j c", j=PACK
                     ),
                 )
-                shifted_v[2 * g + 2] = v_again
+                shifted_v[2 * g] = v_again
 
         ident_f32 = keep.tile([P, P], F32, name="ident_f32")
         make_identity(nc, ident_f32[:])
@@ -109,27 +108,32 @@ def tile_slidingselfattention_pa_t_kernel(tc, qkv, out):
         v_codes = {}
         v_scales = {}
 
-        def transpose_rows(g, first_word, is_key):
-            words = raw[g][:].bitcast(F32)
-            flipped = psum_x.tile([P, PACK, P], F32, tag="flipped")
+        flipped = {}
+
+        def transpose_rows(item):
+            if item >= 2 * N_LOADS:
+                return
+            words = raw[item // 2][:].bitcast(F32)
+            first_word = (item % 2) * PAIRS
+            flipped[item] = psum_x.tile([P, PACK, P], F32, name="flipped")
             for j in range(PACK):
                 nc.tensor.transpose(
-                    flipped[:, j, :], words[:, j, first_word : first_word + PAIRS], ident_f32[:]
+                    flipped[item][:, j, :], words[:, j, first_word : first_word + PAIRS], ident_f32[:]
                 )
-            if is_key:
+
+        def copy_rows(item):
+            if item >= 2 * N_LOADS:
+                return
+            if item % 2 == 0:
                 nc.vector.tensor_copy(
-                    out=k_t[g][:].rearrange("w (c t r) -> w c t r", t=PACK, r=QUARTER),
-                    in_=flipped[:].rearrange("w t (c r) -> w c t r", r=QUARTER),
+                    out=q_t[item // 2][:].rearrange("w (p j) -> w p j", j=PACK),
+                    in_=flipped[item][:].rearrange("w j p -> w p j"),
                 )
             else:
                 nc.vector.tensor_copy(
-                    out=q_t[g][:].rearrange("w (p j) -> w p j", j=PACK),
-                    in_=flipped[:].rearrange("w j p -> w p j"),
+                    out=k_t[item // 2][:].rearrange("w (c t r) -> w c t r", t=PACK, r=QUARTER),
+                    in_=flipped[item][:].rearrange("w t (c r) -> w c t r", r=QUARTER),
                 )
-
-        def transpose_next(item):
-            if item < 2 * N_LOADS:
-                transpose_rows(item // 2, (item % 2) * PAIRS, item % 2 == 1)
 
         grouped_v = {}
 
@@ -262,31 +266,33 @@ def tile_slidingselfattention_pa_t_kernel(tc, qkv, out):
             return 0 <= n < N_BLOCKS
 
         with tc.manual_schedule():
-            transpose_next(0)
-            transpose_next(1)
-            next_item = 2
-            for k in range(N_BLOCKS + 3):
+            transpose_rows(0)
+            copy_rows(0)
+            transpose_rows(1)
+            copy_rows(1)
+            transpose_rows(2)
+            for k in range(N_BLOCKS + 4):
+                if is_block(k - 4):
+                    divide_and_store(k - 4)
+                if is_block(k - 3):
+                    quantise_e(k - 3)
                 if is_block(k - 2):
-                    group_e(k - 2)
+                    invert_row_sums(k - 2)
+                copy_rows(k + 2)
                 if is_block(k):
                     score(k, 0)
                     score(k, 1)
-                if is_block(k - 2):
-                    quantise_e(k - 2)
-                if is_block(k):
-                    scale_row_max(k)
                 if is_block(k - 1):
-                    invert_row_sums(k - 1)
+                    exponentials(k - 1)
                 if is_block(k - 3):
                     weighted_sum(k - 3)
-                    divide_and_store(k - 3)
-                if is_block(k):
-                    exponentials(k)
+                transpose_rows(k + 3)
+                if is_block(k - 2):
+                    group_e(k - 2)
                 if 1 <= k < N_BLOCKS:
                     quantise_v(k)
-                while next_item <= k + AHEAD:
-                    transpose_next(next_item)
-                    next_item += 1
+                if is_block(k):
+                    scale_row_max(k)
                 if 1 <= k + 1 < N_BLOCKS:
                     group_v(k + 1)
                 if is_block(k - 1):

@@ -40,6 +40,7 @@ def tile_slidingselfattention_pa_t_kernel(tc, qkv, out):
         keep = ctx.enter_context(tc.tile_pool(name="keep", bufs=1))
         work = ctx.enter_context(tc.tile_pool(name="work", bufs=3))
         small = ctx.enter_context(tc.tile_pool(name="small", bufs=6))
+        stage_v = ctx.enter_context(tc.tile_pool(name="stage_v", bufs=2))
         psum_s = ctx.enter_context(tc.psum_pool(name="psum_s", bufs=4))
         psum_x = ctx.enter_context(tc.psum_pool(name="psum_x", bufs=1))
         psum_t = ctx.enter_context(tc.psum_pool(name="psum_t", bufs=2))
@@ -139,10 +140,10 @@ def tile_slidingselfattention_pa_t_kernel(tc, qkv, out):
 
         def group_v(n):
             rows = shifted_v[n][:] if n in shifted_v else raw[n // 2][:, :, 2 * D : 3 * D]
-            grouped_v[n] = work.tile([P, D, PACK], BF16, name="grouped_v", align_bytes=64)
-            nc.vector.tensor_copy(
-                out=grouped_v[n][:].rearrange("p (c i) t -> p c t i", i=4),
-                in_=rows.rearrange("p t (c i) -> p c t i", i=4),
+            grouped_v[n] = stage_v.tile([P, D, PACK], BF16, name="grouped_v", align_bytes=64)
+            nc.gpsimd.tensor_scalar(
+                out=grouped_v[n][:], in0=rows.rearrange("p t d -> p d t"),
+                scalar1=1.0, scalar2=0.0, op0=ALU.mult, op1=ALU.add,
             )
 
         def quantise_v(n):
@@ -271,6 +272,7 @@ def tile_slidingselfattention_pa_t_kernel(tc, qkv, out):
             transpose_rows(1)
             copy_rows(1)
             transpose_rows(2)
+            group_v(1)
             for k in range(N_BLOCKS + 4):
                 if is_block(k - 4):
                     divide_and_store(k - 4)
@@ -278,6 +280,10 @@ def tile_slidingselfattention_pa_t_kernel(tc, qkv, out):
                     quantise_e(k - 3)
                 if is_block(k - 2):
                     invert_row_sums(k - 2)
+                if 1 <= k < N_BLOCKS:
+                    quantise_v(k)
+                if k + 2 < N_BLOCKS:
+                    group_v(k + 2)
                 copy_rows(k + 2)
                 if is_block(k):
                     score(k, 0)
@@ -289,11 +295,7 @@ def tile_slidingselfattention_pa_t_kernel(tc, qkv, out):
                 transpose_rows(k + 3)
                 if is_block(k - 2):
                     group_e(k - 2)
-                if 1 <= k < N_BLOCKS:
-                    quantise_v(k)
                 if is_block(k):
                     scale_row_max(k)
-                if 1 <= k + 1 < N_BLOCKS:
-                    group_v(k + 1)
                 if is_block(k - 1):
                     transpose_e(k - 1)

@@ -42,9 +42,8 @@ def tile_slidingselfattention_pa_t_kernel(tc, qkv, out):
         small = ctx.enter_context(tc.tile_pool(name="small", bufs=6))
         stage_v = ctx.enter_context(tc.tile_pool(name="stage_v", bufs=2))
         psum_s = ctx.enter_context(tc.psum_pool(name="psum_s", bufs=4))
-        psum_x = ctx.enter_context(tc.psum_pool(name="psum_x", bufs=1))
         psum_t = ctx.enter_context(tc.psum_pool(name="psum_t", bufs=2))
-        psum_o = ctx.enter_context(tc.psum_pool(name="psum_o", bufs=1))
+        psum_b = ctx.enter_context(tc.psum_pool(name="psum_b", bufs=2))
 
         raw = []
         shifted_v = {}
@@ -116,22 +115,22 @@ def tile_slidingselfattention_pa_t_kernel(tc, qkv, out):
                 return
             words = raw[item // 2][:].bitcast(F32)
             first_word = (item % 2) * PAIRS
-            flipped[item] = psum_x.tile([P, PACK, P], F32, name="flipped")
+            flipped[item] = psum_b.tile([P, PACK, P], F32, name="flipped", tag="bank")
             for j in range(PACK):
                 nc.tensor.transpose(
                     flipped[item][:, j, :], words[:, j, first_word : first_word + PAIRS], ident_f32[:]
                 )
 
-        def copy_rows(item):
+        def copy_rows(item, copy):
             if item >= 2 * N_LOADS:
                 return
             if item % 2 == 0:
-                nc.vector.tensor_copy(
+                copy(
                     out=q_t[item // 2][:].rearrange("w (p j) -> w p j", j=PACK),
                     in_=flipped[item][:].rearrange("w j p -> w p j"),
                 )
             else:
-                nc.vector.tensor_copy(
+                copy(
                     out=k_t[item // 2][:].rearrange("w (c t r) -> w c t r", t=PACK, r=QUARTER),
                     in_=flipped[item][:].rearrange("w t (c r) -> w c t r", r=QUARTER),
                 )
@@ -234,7 +233,7 @@ def tile_slidingselfattention_pa_t_kernel(tc, qkv, out):
 
         def weighted_sum(n):
             window = max(n, 1)
-            summed[n] = psum_o.tile([P, HALVES, D], F32, name="summed")
+            summed[n] = psum_b.tile([P, HALVES, D], F32, name="summed", tag="bank")
             for h in range(HALVES):
                 nc.tensor.matmul_mx(
                     out=summed[n][:, h, :],
@@ -251,13 +250,19 @@ def tile_slidingselfattention_pa_t_kernel(tc, qkv, out):
             inverse[n] = small.tile([P, HALVES], F32, name="inverse")
             nc.vector.reciprocal(out=inverse[n][:], in_=row_sums[n][:])
 
-        def divide_and_store(n):
+        def divide_and_store(n, on_vector):
             result = work.tile([P, HALVES, D], F32, name="result")
             for h in range(HALVES):
-                nc.scalar.activation(
-                    out=result[:, h, :], in_=summed[n][:, h, :], func=ACT.Copy,
-                    scale=inverse[n][:, h : h + 1],
-                )
+                if on_vector:
+                    nc.vector.tensor_scalar(
+                        out=result[:, h, :], in0=summed[n][:, h, :],
+                        scalar1=inverse[n][:, h : h + 1], scalar2=None, op0=ALU.mult,
+                    )
+                else:
+                    nc.scalar.activation(
+                        out=result[:, h, :], in_=summed[n][:, h, :], func=ACT.Copy,
+                        scale=inverse[n][:, h : h + 1],
+                    )
             nc.sync.dma_start(
                 out=out[0, n * BLOCK : (n + 1) * BLOCK, :].rearrange("(h p) d -> p h d", h=HALVES),
                 in_=result[:],
@@ -268,14 +273,14 @@ def tile_slidingselfattention_pa_t_kernel(tc, qkv, out):
 
         with tc.manual_schedule():
             transpose_rows(0)
-            copy_rows(0)
             transpose_rows(1)
-            copy_rows(1)
+            copy_rows(0, nc.vector.tensor_copy)
+            copy_rows(1, nc.scalar.copy)
             transpose_rows(2)
             group_v(1)
             for k in range(N_BLOCKS + 4):
                 if is_block(k - 4):
-                    divide_and_store(k - 4)
+                    divide_and_store(k - 4, on_vector=(k >= N_BLOCKS))
                 if is_block(k - 3):
                     quantise_e(k - 3)
                 if is_block(k - 2):
@@ -284,7 +289,7 @@ def tile_slidingselfattention_pa_t_kernel(tc, qkv, out):
                     quantise_v(k)
                 if k + 2 < N_BLOCKS:
                     group_v(k + 2)
-                copy_rows(k + 2)
+                copy_rows(k + 2, nc.vector.tensor_copy)
                 if is_block(k):
                     score(k, 0)
                     score(k, 1)

@@ -17,6 +17,7 @@ PACK = 4
 SEQ = 4096
 D = 256
 PAIRS = D // 2
+DUO = 2
 BLOCK = 256
 HALVES = BLOCK // P
 N_BLOCKS = SEQ // BLOCK
@@ -80,14 +81,11 @@ def tile_slidingselfattention_pa_t_kernel(tc, qkv, out):
             base=0, pattern=[[-1, CHUNK]], channel_multiplier=1,
         )
         mask = keep.tile([P, 2, CHUNK], BF16, name="mask")
-        nc.vector.tensor_copy(
-            out=mask[:].rearrange("i m (t r) -> i m t r", t=PACK),
-            in_=mask_rows[:].rearrange("i m (r t) -> i m t r", t=PACK),
-        )
+        nc.vector.tensor_copy(out=mask[:], in_=mask_rows[:])
 
-        e_first = [keep.tile([P, PACK, P], BF16, name="e_first%d" % h) for h in range(HALVES)]
+        e_first = [keep.tile([P, DUO, P, DUO], BF16, name="e_first%d" % h) for h in range(HALVES)]
         e_ring = [
-            [keep.tile([P, PACK, P], BF16, name="e_ring%d_%d" % (h, i)) for i in range(E_RING)]
+            [keep.tile([P, DUO, P, DUO], BF16, name="e_ring%d_%d" % (h, i)) for i in range(E_RING)]
             for h in range(HALVES)
         ]
         for h in range(HALVES):
@@ -124,16 +122,11 @@ def tile_slidingselfattention_pa_t_kernel(tc, qkv, out):
         def copy_rows(item, copy):
             if item >= 2 * N_LOADS:
                 return
-            if item % 2 == 0:
-                copy(
-                    out=q_t[item // 2][:].rearrange("w (p j) -> w p j", j=PACK),
-                    in_=flipped[item][:].rearrange("w j p -> w p j"),
-                )
-            else:
-                copy(
-                    out=k_t[item // 2][:].rearrange("w (c t r) -> w c t r", t=PACK, r=QUARTER),
-                    in_=flipped[item][:].rearrange("w t (c r) -> w c t r", r=QUARTER),
-                )
+            target = (q_t if item % 2 == 0 else k_t)[item // 2]
+            copy(
+                out=target[:].rearrange("w (p j) -> w p j", j=PACK),
+                in_=flipped[item][:].rearrange("w j p -> w p j"),
+            )
 
         grouped_v = {}
 
@@ -170,22 +163,23 @@ def tile_slidingselfattention_pa_t_kernel(tc, qkv, out):
 
         def score(n, h):
             u = HALVES * n + h
-            s = psum_s.tile([P, SLOTS, CHUNK], F32, name="s")
+            s = psum_s.tile([P, DUO, SLOTS, QUARTER, DUO], F32, name="s")
             for slot in range(first_slot(u), SLOTS):
+                key_order = s[:, :, slot, :, :].rearrange("i u r b -> i r u b")
                 if slot != 1:
                     nc.tensor.matmul(
-                        out=s[:, slot, :], lhsT=ident_bf16[:], rhs=mask[:, slot // 2, :],
+                        out=key_order, lhsT=ident_bf16[:], rhs=mask[:, slot // 2, :],
                         start=True, stop=False,
                     )
                 for f in range(2):
                     nc.tensor.matmul(
-                        out=s[:, slot, :], lhsT=q_columns(u, f), rhs=k_columns(u - 2 + slot, f),
+                        out=key_order, lhsT=q_columns(u, f), rhs=k_columns(u - 2 + slot, f),
                         start=(slot == 1 and f == 0), stop=(f == 1),
                     )
             if h == 0:
                 row_max[n] = small.tile([P, HALVES], F32, name="row_max")
             nc.vector.reduce_max(
-                out=row_max[n][:, h : h + 1], in_=s[:, first_slot(u) : SLOTS, :], axis=AXIS.XY
+                out=row_max[n][:, h : h + 1], in_=s[:, :, first_slot(u) : SLOTS, :, :].rearrange("i u k r b -> i u (k r b)"), axis=AXIS.XY
             )
             scores[n, h] = s
 
@@ -204,23 +198,27 @@ def tile_slidingselfattention_pa_t_kernel(tc, qkv, out):
                 seen = SLOTS - first
                 quarter = u - 2 + first - HALVES * max(n - 1, 0)
                 nc.scalar.activation(
-                    out=e_tiles[n][h][:, :, quarter * QUARTER : (quarter + seen) * QUARTER].rearrange(
-                        "i t (k r) -> i t k r", r=QUARTER
+                    out=e_tiles[n][h][:, :, quarter * QUARTER : (quarter + seen) * QUARTER, :].rearrange(
+                        "i u p b -> i u (p b)"
                     ),
-                    in_=scores[n, h][:, first:SLOTS, :].rearrange("i k (t r) -> i t k r", t=PACK),
+                    in_=scores[n, h][:, :, first:SLOTS, :, :].rearrange("i u k r b -> i u (k r b)"),
                     func=ACT.Exp, bias=shifts[n][:, h : h + 1], scale=SCALE,
                     accum_out=row_sums[n][:, h : h + 1],
                 )
 
         def transpose_e(n):
-            flipped_e[n] = psum_t.tile([P, HALVES, PACK, P], BF16, name="flipped_e")
+            flipped_e[n] = psum_t.tile([P, HALVES, DUO, P], F32, name="flipped_e")
             for h in range(HALVES):
-                for t in range(PACK):
-                    nc.tensor.transpose(flipped_e[n][:, h, t, :], e_tiles[n][h][:, t, :], ident_bf16[:])
+                words = e_tiles[n][h][:].rearrange("i u p b -> i (u p b)").bitcast(F32)
+                for u in range(DUO):
+                    nc.tensor.transpose(flipped_e[n][:, h, u, :], words[:, u * P : (u + 1) * P], ident_f32[:])
 
         def group_e(n):
-            grouped_e[n] = work.tile([P, HALVES, P, PACK], BF16, name="grouped_e", align_bytes=64)
-            nc.scalar.copy(out=grouped_e[n][:], in_=flipped_e[n][:].rearrange("p h t i -> p h i t"))
+            grouped_e[n] = work.tile([P, HALVES * P * PACK], BF16, name="grouped_e", align_bytes=64)
+            nc.scalar.copy(
+                out=grouped_e[n][:].bitcast(F32).rearrange("p (h i u) -> p h i u", h=HALVES, u=DUO),
+                in_=flipped_e[n][:].rearrange("p h u i -> p h i u"),
+            )
 
         def quantise_e(n):
             e_codes[n] = work.tile([P, HALVES * P], U32, name="e_codes", align_bytes=64)
@@ -228,7 +226,7 @@ def tile_slidingselfattention_pa_t_kernel(tc, qkv, out):
             nc.vector.quantize_mx(
                 out=e_codes[n][:].bitcast(FP8X4),
                 scales=e_scales[n][:],
-                in_=grouped_e[n][:].rearrange("p h i t -> p (h i t)"),
+                in_=grouped_e[n][:],
             )
 
         def weighted_sum(n):

@@ -6,6 +6,7 @@ from concourse.masks import make_identity
 F32 = mybir.dt.float32
 BF16 = mybir.dt.bfloat16
 U32 = mybir.dt.uint32
+I32 = mybir.dt.int32
 U8 = mybir.dt.uint8
 FP8X4 = mybir.dt.float8_e4m3fn_x4
 ACT = mybir.ActivationFunctionType
@@ -41,13 +42,12 @@ def tile_slidingselfattention_pa_t_kernel(tc, qkv, out):
         keep = ctx.enter_context(tc.tile_pool(name="keep", bufs=1))
         work = ctx.enter_context(tc.tile_pool(name="work", bufs=3))
         small = ctx.enter_context(tc.tile_pool(name="small", bufs=6))
-        stage_v = ctx.enter_context(tc.tile_pool(name="stage_v", bufs=2))
+        stage_v = ctx.enter_context(tc.tile_pool(name="stage_v", bufs=1))
         psum_s = ctx.enter_context(tc.psum_pool(name="psum_s", bufs=4))
         psum_t = ctx.enter_context(tc.psum_pool(name="psum_t", bufs=2))
         psum_b = ctx.enter_context(tc.psum_pool(name="psum_b", bufs=2))
 
         raw = []
-        shifted_v = {}
         for g in range(N_LOADS):
             raw_g = keep.tile([P, PACK, 3 * D], BF16, name="raw%d" % g)
             nc.sync.dma_start(
@@ -55,16 +55,6 @@ def tile_slidingselfattention_pa_t_kernel(tc, qkv, out):
                 in_=qkv[0, g * ROWS : (g + 1) * ROWS, :].rearrange("(p j) c -> p j c", j=PACK),
             )
             raw.append(raw_g)
-            if g >= 1:
-                first_key = g * ROWS - BLOCK
-                v_again = keep.tile([P, PACK, D], BF16, name="shifted_v%d" % g)
-                nc.sync.dma_start(
-                    out=v_again[:],
-                    in_=qkv[0, first_key : first_key + WINDOW, 2 * D : 3 * D].rearrange(
-                        "(p j) c -> p j c", j=PACK
-                    ),
-                )
-                shifted_v[2 * g] = v_again
 
         ident_f32 = keep.tile([P, P], F32, name="ident_f32")
         make_identity(nc, ident_f32[:])
@@ -93,15 +83,15 @@ def tile_slidingselfattention_pa_t_kernel(tc, qkv, out):
                 nc.vector.memset(e_tile[:], 0.0)
 
         q_t = [keep.tile([P, ROWS], F32, name="q_t%d" % g) for g in range(N_LOADS)]
-        k_t = [keep.tile([P, ROWS], F32, name="k_t%d" % g) for g in range(N_LOADS)]
+        k_t = keep.tile([P, SEQ], F32, name="k_t")
 
         def q_columns(u, f):
             halves = q_t[u // LOAD_CHUNKS][:].bitcast(BF16).rearrange("w (c i f) -> w c i f", c=LOAD_CHUNKS, f=2)
             return halves[:, u % LOAD_CHUNKS, :, f]
 
-        def k_columns(c, f):
-            chunks = k_t[c // LOAD_CHUNKS][:].bitcast(BF16).rearrange("w (c x f) -> w c x f", c=LOAD_CHUNKS, f=2)
-            return chunks[:, c % LOAD_CHUNKS, :, f]
+        def k_columns(first, last, f):
+            keys = k_t[:].bitcast(BF16).rearrange("w (x f) -> w x f", f=2)
+            return keys[:, first * CHUNK : (last + 1) * CHUNK, f]
 
         v_codes = {}
         v_scales = {}
@@ -122,30 +112,44 @@ def tile_slidingselfattention_pa_t_kernel(tc, qkv, out):
         def copy_rows(item, copy):
             if item >= 2 * N_LOADS:
                 return
-            target = (q_t if item % 2 == 0 else k_t)[item // 2]
+            g = item // 2
+            target = q_t[g][:] if item % 2 == 0 else k_t[:, g * ROWS : (g + 1) * ROWS]
             copy(
-                out=target[:].rearrange("w (p j) -> w p j", j=PACK),
+                out=target.rearrange("w (p j) -> w p j", j=PACK),
                 in_=flipped[item][:].rearrange("w j p -> w p j"),
             )
 
         grouped_v = {}
 
-        def group_v(n):
-            rows = shifted_v[n][:] if n in shifted_v else raw[n // 2][:, :, 2 * D : 3 * D]
-            grouped_v[n] = stage_v.tile([P, D, PACK], BF16, name="grouped_v", align_bytes=64)
+        def group_v(g):
+            grouped_v[g] = stage_v.tile([P, D, PACK], BF16, name="grouped_v", align_bytes=64)
             nc.gpsimd.tensor_scalar(
-                out=grouped_v[n][:], in0=rows.rearrange("p t d -> p d t"),
+                out=grouped_v[g][:], in0=raw[g][:, :, 2 * D : 3 * D].rearrange("p t d -> p d t"),
                 scalar1=1.0, scalar2=0.0, op0=ALU.mult, op1=ALU.add,
             )
 
-        def quantise_v(n):
+        def operand_tiles(n):
             v_codes[n] = keep.tile([P, D], U32, name="v_codes%d" % n, align_bytes=64)
             v_scales[n] = keep.tile([P, D], U8, name="v_scales%d" % n, align_bytes=64)
+
+        def quantise_v(g):
+            n = 2 * g + 1
+            operand_tiles(n)
             nc.vector.quantize_mx(
                 out=v_codes[n][:].bitcast(FP8X4),
                 scales=v_scales[n][:],
-                in_=grouped_v[n][:].rearrange("p d t -> p (d t)"),
+                in_=grouped_v[g][:].rearrange("p d t -> p (d t)"),
             )
+
+        def assemble_v(n):
+            operand_tiles(n)
+            for made in (v_codes, v_scales):
+                for low, source in ((0, n - 1), (P // 2, n + 1)):
+                    high = P // 2 - low
+                    nc.sync.dma_start(
+                        out=made[n][low : low + P // 2, :].bitcast(I32),
+                        in_=made[source][high : high + P // 2, :].bitcast(I32),
+                    )
 
         scores = {}
         row_max = {}
@@ -164,18 +168,25 @@ def tile_slidingselfattention_pa_t_kernel(tc, qkv, out):
         def score(n, h):
             u = HALVES * n + h
             s = psum_s.tile([P, DUO, SLOTS, QUARTER, DUO], F32, name="s")
-            for slot in range(first_slot(u), SLOTS):
-                key_order = s[:, :, slot, :, :].rearrange("i u r b -> i r u b")
-                if slot != 1:
+            first = first_slot(u)
+
+            def columns(a, b):
+                return s[:, :, a:b, :, :].rearrange("i u k r b -> i (k r) u b")
+
+            nc.tensor.matmul(
+                out=columns(first, SLOTS), lhsT=q_columns(u, 0), rhs=k_columns(u - 2 + first, u, 0),
+                start=True, stop=False,
+            )
+            for slot in (0, 2):
+                if slot >= first:
                     nc.tensor.matmul(
-                        out=key_order, lhsT=ident_bf16[:], rhs=mask[:, slot // 2, :],
-                        start=True, stop=False,
+                        out=columns(slot, slot + 1), lhsT=ident_bf16[:], rhs=mask[:, slot // 2, :],
+                        start=False, stop=False,
                     )
-                for f in range(2):
-                    nc.tensor.matmul(
-                        out=key_order, lhsT=q_columns(u, f), rhs=k_columns(u - 2 + slot, f),
-                        start=(slot == 1 and f == 0), stop=(f == 1),
-                    )
+            nc.tensor.matmul(
+                out=columns(first, SLOTS), lhsT=q_columns(u, 1), rhs=k_columns(u - 2 + first, u, 1),
+                start=False, stop=True,
+            )
             if h == 0:
                 row_max[n] = small.tile([P, HALVES], F32, name="row_max")
             nc.vector.reduce_max(
@@ -275,7 +286,7 @@ def tile_slidingselfattention_pa_t_kernel(tc, qkv, out):
             copy_rows(0, nc.vector.tensor_copy)
             copy_rows(1, nc.scalar.copy)
             transpose_rows(2)
-            group_v(1)
+            group_v(0)
             for k in range(N_BLOCKS + 4):
                 if is_block(k - 4):
                     divide_and_store(k - 4, on_vector=(k >= N_BLOCKS))
@@ -283,10 +294,14 @@ def tile_slidingselfattention_pa_t_kernel(tc, qkv, out):
                     quantise_e(k - 3)
                 if is_block(k - 2):
                     invert_row_sums(k - 2)
-                if 1 <= k < N_BLOCKS:
-                    quantise_v(k)
-                if k + 2 < N_BLOCKS:
-                    group_v(k + 2)
+                if k == 1:
+                    quantise_v(0)
+                    group_v(1)
+                elif k % 2 == 0 and 1 <= k // 2 < N_LOADS:
+                    quantise_v(k // 2)
+                    assemble_v(k)
+                    if k // 2 + 1 < N_LOADS:
+                        group_v(k // 2 + 1)
                 copy_rows(k + 2, nc.vector.tensor_copy)
                 if is_block(k):
                     score(k, 0)

@@ -32,6 +32,7 @@ SLOTS = 3
 SCALE = 1.0 / 16.0
 HIDDEN = -10000.0 / SCALE
 E_RING = 3
+FIRST_PACK = BLOCK // P
 
 FLOPS = 2 * (2 * SEQ * WINDOW * D)
 
@@ -42,36 +43,43 @@ def tile_slidingselfattention_pa_t_kernel(tc, qkv, out):
         keep = ctx.enter_context(tc.tile_pool(name="keep", bufs=1))
         work = ctx.enter_context(tc.tile_pool(name="work", bufs=3))
         small = ctx.enter_context(tc.tile_pool(name="small", bufs=6))
+        results = ctx.enter_context(tc.tile_pool(name="results", bufs=6))
         stage_v = ctx.enter_context(tc.tile_pool(name="stage_v", bufs=1))
         psum_s = ctx.enter_context(tc.psum_pool(name="psum_s", bufs=4))
         psum_t = ctx.enter_context(tc.psum_pool(name="psum_t", bufs=2))
         psum_b = ctx.enter_context(tc.psum_pool(name="psum_b", bufs=2))
 
-        raw = []
-        for g in range(N_LOADS):
-            raw_g = keep.tile([P, PACK, 3 * D], BF16, name="raw%d" % g)
+        def load(first, pack, left, right, name):
+            rows = keep.tile([P, pack, right - left], BF16, name=name)
             nc.sync.dma_start(
-                out=raw_g[:],
-                in_=qkv[0, g * ROWS : (g + 1) * ROWS, :].rearrange("(p j) c -> p j c", j=PACK),
+                out=rows[:],
+                in_=qkv[0, first : first + pack * P, left:right].rearrange("(p j) c -> p j c", j=pack),
             )
-            raw.append(raw_g)
+            return rows
+
+        qk_rows = [load(n * BLOCK, FIRST_PACK, 0, 2 * D, "first_rows%d" % n) for n in range(HALVES)]
+        raw = {}
+        v_rows = {}
+        for g in range(1, N_LOADS):
+            raw[g] = load(g * ROWS, PACK, 0, 3 * D, "raw%d" % g)
+            v_rows[g] = raw[g][:, :, 2 * D :]
+            if g == 1:
+                v_rows[0] = load(0, PACK, 2 * D, 3 * D, "v_rows0")[:]
 
         ident_f32 = keep.tile([P, P], F32, name="ident_f32")
         make_identity(nc, ident_f32[:])
         ident_bf16 = keep.tile([P, P], BF16, name="ident_bf16")
         make_identity(nc, ident_bf16[:])
-        mask_rows = keep.tile([P, 2, CHUNK], F32, name="mask_rows")
-        nc.gpsimd.memset(mask_rows[:], 0.0)
+        mask = keep.tile([P, 2, CHUNK], BF16, name="mask")
+        nc.gpsimd.memset(mask[:], 0.0)
         nc.gpsimd.affine_select(
-            out=mask_rows[:, 0, :], in_=mask_rows[:, 0, :], compare_op=ALU.is_ge, fill=HIDDEN,
+            out=mask[:, 0, :], in_=mask[:, 0, :], compare_op=ALU.is_ge, fill=HIDDEN,
             base=0, pattern=[[1, CHUNK]], channel_multiplier=-1,
         )
         nc.gpsimd.affine_select(
-            out=mask_rows[:, 1, :], in_=mask_rows[:, 1, :], compare_op=ALU.is_ge, fill=HIDDEN,
+            out=mask[:, 1, :], in_=mask[:, 1, :], compare_op=ALU.is_ge, fill=HIDDEN,
             base=0, pattern=[[-1, CHUNK]], channel_multiplier=1,
         )
-        mask = keep.tile([P, 2, CHUNK], BF16, name="mask")
-        nc.vector.tensor_copy(out=mask[:], in_=mask_rows[:])
 
         e_first = [keep.tile([P, DUO, P, DUO], BF16, name="e_first%d" % h) for h in range(HALVES)]
         e_ring = [
@@ -79,44 +87,40 @@ def tile_slidingselfattention_pa_t_kernel(tc, qkv, out):
             for h in range(HALVES)
         ]
         for h in range(HALVES):
-            for e_tile in [e_first[h]] + e_ring[h]:
-                nc.vector.memset(e_tile[:], 0.0)
+            nc.vector.memset(e_first[h][:, :, (h + 1) * QUARTER :, :], 0.0)
+            hidden = (SLOTS * (1 - h)) * QUARTER
+            for e_tile in e_ring[h]:
+                nc.vector.memset(e_tile[:, :, hidden : hidden + QUARTER, :], 0.0)
 
-        q_t = [keep.tile([P, ROWS], F32, name="q_t%d" % g) for g in range(N_LOADS)]
-        k_t = keep.tile([P, SEQ], F32, name="k_t")
+        turned = [keep.tile([P, SEQ], F32, name="q_t"), keep.tile([P, SEQ], F32, name="k_t")]
 
-        def q_columns(u, f):
-            halves = q_t[u // LOAD_CHUNKS][:].bitcast(BF16).rearrange("w (c i f) -> w c i f", c=LOAD_CHUNKS, f=2)
-            return halves[:, u % LOAD_CHUNKS, :, f]
-
-        def k_columns(first, last, f):
-            keys = k_t[:].bitcast(BF16).rearrange("w (x f) -> w x f", f=2)
-            return keys[:, first * CHUNK : (last + 1) * CHUNK, f]
+        def columns_of(which, first, last, f):
+            rows = turned[which][:].bitcast(BF16).rearrange("w (x f) -> w x f", f=2)
+            return rows[:, first * CHUNK : (last + 1) * CHUNK, f]
 
         v_codes = {}
         v_scales = {}
 
         flipped = {}
 
-        def transpose_rows(item):
-            if item >= 2 * N_LOADS:
-                return
-            words = raw[item // 2][:].bitcast(F32)
-            first_word = (item % 2) * PAIRS
-            flipped[item] = psum_b.tile([P, PACK, P], F32, name="flipped", tag="bank")
-            for j in range(PACK):
+        def pack_of(first):
+            return FIRST_PACK if first < ROWS else PACK
+
+        def transpose_rows(first, which, pool, tag):
+            pack = pack_of(first)
+            rows = qk_rows[first // BLOCK] if first < ROWS else raw[first // ROWS]
+            words = rows[:].bitcast(F32)
+            flipped[first, which] = pool.tile([P, pack, P], F32, name="flipped", tag=tag)
+            for j in range(pack):
                 nc.tensor.transpose(
-                    flipped[item][:, j, :], words[:, j, first_word : first_word + PAIRS], ident_f32[:]
+                    flipped[first, which][:, j, :], words[:, j, which * PAIRS : (which + 1) * PAIRS], ident_f32[:]
                 )
 
-        def copy_rows(item, copy):
-            if item >= 2 * N_LOADS:
-                return
-            g = item // 2
-            target = q_t[g][:] if item % 2 == 0 else k_t[:, g * ROWS : (g + 1) * ROWS]
+        def copy_rows(first, which, copy):
+            pack = pack_of(first)
             copy(
-                out=target.rearrange("w (p j) -> w p j", j=PACK),
-                in_=flipped[item][:].rearrange("w j p -> w p j"),
+                out=turned[which][:, first : first + pack * P].rearrange("w (p j) -> w p j", j=pack),
+                in_=flipped[first, which][:].rearrange("w j p -> w p j"),
             )
 
         grouped_v = {}
@@ -124,7 +128,7 @@ def tile_slidingselfattention_pa_t_kernel(tc, qkv, out):
         def group_v(g):
             grouped_v[g] = stage_v.tile([P, D, PACK], BF16, name="grouped_v", align_bytes=64)
             nc.gpsimd.tensor_scalar(
-                out=grouped_v[g][:], in0=raw[g][:, :, 2 * D : 3 * D].rearrange("p t d -> p d t"),
+                out=grouped_v[g][:], in0=v_rows[g].rearrange("p t d -> p d t"),
                 scalar1=1.0, scalar2=0.0, op0=ALU.mult, op1=ALU.add,
             )
 
@@ -155,26 +159,26 @@ def tile_slidingselfattention_pa_t_kernel(tc, qkv, out):
         row_max = {}
         shifts = {}
         row_sums = {}
-        e_tiles = {}
         flipped_e = {}
         grouped_e = {}
         e_codes = {}
         e_scales = {}
         summed = {}
+        inverse = {}
 
         def first_slot(u):
             return max(0, SLOTS - 1 - u)
 
         def score(n, h):
             u = HALVES * n + h
-            s = psum_s.tile([P, DUO, SLOTS, QUARTER, DUO], F32, name="s")
+            s = psum_s.tile([P, DUO, SLOTS, QUARTER, DUO], F32, name="s", tag="s")
             first = first_slot(u)
 
             def columns(a, b):
                 return s[:, :, a:b, :, :].rearrange("i u k r b -> i (k r) u b")
 
             nc.tensor.matmul(
-                out=columns(first, SLOTS), lhsT=q_columns(u, 0), rhs=k_columns(u - 2 + first, u, 0),
+                out=columns(first, SLOTS), lhsT=columns_of(0, u, u, 0), rhs=columns_of(1, u - 2 + first, u, 0),
                 start=True, stop=False,
             )
             for slot in (0, 2):
@@ -184,32 +188,42 @@ def tile_slidingselfattention_pa_t_kernel(tc, qkv, out):
                         start=False, stop=False,
                     )
             nc.tensor.matmul(
-                out=columns(first, SLOTS), lhsT=q_columns(u, 1), rhs=k_columns(u - 2 + first, u, 1),
+                out=columns(first, SLOTS), lhsT=columns_of(0, u, u, 1), rhs=columns_of(1, u - 2 + first, u, 1),
                 start=False, stop=True,
-            )
-            if h == 0:
-                row_max[n] = small.tile([P, HALVES], F32, name="row_max")
-            nc.vector.reduce_max(
-                out=row_max[n][:, h : h + 1], in_=s[:, :, first_slot(u) : SLOTS, :, :].rearrange("i u k r b -> i u (k r b)"), axis=AXIS.XY
             )
             scores[n, h] = s
 
-        def scale_row_max(n):
-            shifts[n] = small.tile([P, HALVES], F32, name="shift")
-            nc.vector.tensor_scalar(
-                out=shifts[n][:], in0=row_max[n][:], scalar1=-SCALE, scalar2=None, op0=ALU.mult
+        def take_max(n, h):
+            if h == 0:
+                row_max[n] = small.tile([P, HALVES], F32, name="row_max")
+            s = scores[n, h]
+            nc.vector.reduce_max(
+                out=row_max[n][:, h : h + 1],
+                in_=s[:, :, first_slot(HALVES * n + h) : SLOTS, :, :].rearrange("i u k r b -> i u (k r b)"),
+                axis=AXIS.XY,
             )
 
-        def exponentials(n):
-            e_tiles[n] = e_first if n == 0 else [e_ring[h][n % E_RING] for h in range(HALVES)]
-            row_sums[n] = small.tile([P, HALVES], F32, name="row_sums")
-            for h in range(HALVES):
+        def scale_row_max(n, halves):
+            a, b = halves[0], halves[-1] + 1
+            if a == 0:
+                shifts[n] = small.tile([P, HALVES], F32, name="shift")
+            nc.vector.tensor_scalar(
+                out=shifts[n][:, a:b], in0=row_max[n][:, a:b], scalar1=-SCALE, scalar2=None, op0=ALU.mult
+            )
+
+        def e_tile_of(n, h):
+            return e_first[h] if n == 0 else e_ring[h][n % E_RING]
+
+        def exponentials(n, halves):
+            for h in halves:
+                if h == 0:
+                    row_sums[n] = small.tile([P, HALVES], F32, name="row_sums")
                 u = HALVES * n + h
                 first = first_slot(u)
                 seen = SLOTS - first
                 quarter = u - 2 + first - HALVES * max(n - 1, 0)
                 nc.scalar.activation(
-                    out=e_tiles[n][h][:, :, quarter * QUARTER : (quarter + seen) * QUARTER, :].rearrange(
+                    out=e_tile_of(n, h)[:, :, quarter * QUARTER : (quarter + seen) * QUARTER, :].rearrange(
                         "i u p b -> i u (p b)"
                     ),
                     in_=scores[n, h][:, :, first:SLOTS, :, :].rearrange("i u k r b -> i u (k r b)"),
@@ -217,83 +231,110 @@ def tile_slidingselfattention_pa_t_kernel(tc, qkv, out):
                     accum_out=row_sums[n][:, h : h + 1],
                 )
 
-        def transpose_e(n):
-            flipped_e[n] = psum_t.tile([P, HALVES, DUO, P], F32, name="flipped_e")
-            for h in range(HALVES):
-                words = e_tiles[n][h][:].rearrange("i u p b -> i (u p b)").bitcast(F32)
+        def transpose_e(n, halves):
+            flipped_e[n, halves] = psum_t.tile([P, len(halves), DUO, P], F32, name="flipped_e", tag="turned")
+            for i, h in enumerate(halves):
+                words = e_tile_of(n, h)[:].rearrange("i u p b -> i (u p b)").bitcast(F32)
                 for u in range(DUO):
-                    nc.tensor.transpose(flipped_e[n][:, h, u, :], words[:, u * P : (u + 1) * P], ident_f32[:])
+                    nc.tensor.transpose(flipped_e[n, halves][:, i, u, :], words[:, u * P : (u + 1) * P], ident_f32[:])
 
-        def group_e(n):
-            grouped_e[n] = work.tile([P, HALVES * P * PACK], BF16, name="grouped_e", align_bytes=64)
-            nc.scalar.copy(
-                out=grouped_e[n][:].bitcast(F32).rearrange("p (h i u) -> p h i u", h=HALVES, u=DUO),
-                in_=flipped_e[n][:].rearrange("p h u i -> p h i u"),
+        def group_e(n, halves, copy):
+            grouped_e[n, halves] = work.tile([P, len(halves) * P * PACK], BF16, name="grouped_e", align_bytes=64)
+            copy(
+                out=grouped_e[n, halves][:].bitcast(F32).rearrange("p (h i u) -> p h i u", h=len(halves), u=DUO),
+                in_=flipped_e[n, halves][:].rearrange("p h u i -> p h i u"),
             )
 
-        def quantise_e(n):
-            e_codes[n] = work.tile([P, HALVES * P], U32, name="e_codes", align_bytes=64)
-            e_scales[n] = work.tile([P, HALVES * P], U8, name="e_scales", align_bytes=64)
+        def quantise_e(n, halves):
+            e_codes[n, halves] = work.tile([P, len(halves) * P], U32, name="e_codes", align_bytes=64)
+            e_scales[n, halves] = work.tile([P, len(halves) * P], U8, name="e_scales", align_bytes=64)
             nc.vector.quantize_mx(
-                out=e_codes[n][:].bitcast(FP8X4),
-                scales=e_scales[n][:],
-                in_=grouped_e[n][:],
+                out=e_codes[n, halves][:].bitcast(FP8X4),
+                scales=e_scales[n, halves][:],
+                in_=grouped_e[n, halves][:],
             )
 
-        def weighted_sum(n):
+        def weighted_sum(n, halves, pool=psum_b, tag="bank"):
             window = max(n, 1)
-            summed[n] = psum_b.tile([P, HALVES, D], F32, name="summed", tag="bank")
-            for h in range(HALVES):
+            summed[n, halves] = pool.tile([P, len(halves), D], F32, name="summed", tag=tag)
+            for i in range(len(halves)):
                 nc.tensor.matmul_mx(
-                    out=summed[n][:, h, :],
-                    lhsT=e_codes[n][:, h * P : (h + 1) * P].bitcast(FP8X4),
-                    lhsT_scale=e_scales[n][:, h * P : (h + 1) * P],
+                    out=summed[n, halves][:, i, :],
+                    lhsT=e_codes[n, halves][:, i * P : (i + 1) * P].bitcast(FP8X4),
+                    lhsT_scale=e_scales[n, halves][:, i * P : (i + 1) * P],
                     rhs=v_codes[window][:].bitcast(FP8X4),
                     rhs_scale=v_scales[window][:],
                     start=True, stop=True,
                 )
 
-        inverse = {}
-
         def invert_row_sums(n):
             inverse[n] = small.tile([P, HALVES], F32, name="inverse")
             nc.vector.reciprocal(out=inverse[n][:], in_=row_sums[n][:])
 
-        def divide_and_store(n, on_vector):
-            result = work.tile([P, HALVES, D], F32, name="result")
-            for h in range(HALVES):
+        def divide(n, halves, on_vector):
+            result = results.tile([P, len(halves), D], F32, name="result")
+            for i, h in enumerate(halves):
+                source = summed[n, halves][:, i, :]
                 if on_vector:
                     nc.vector.tensor_scalar(
-                        out=result[:, h, :], in0=summed[n][:, h, :],
+                        out=result[:, i, :], in0=source,
                         scalar1=inverse[n][:, h : h + 1], scalar2=None, op0=ALU.mult,
                     )
                 else:
                     nc.scalar.activation(
-                        out=result[:, h, :], in_=summed[n][:, h, :], func=ACT.Copy,
-                        scale=inverse[n][:, h : h + 1],
+                        out=result[:, i, :], in_=source, func=ACT.Copy, scale=inverse[n][:, h : h + 1]
                     )
+            first = n * BLOCK + halves[0] * P
             nc.sync.dma_start(
-                out=out[0, n * BLOCK : (n + 1) * BLOCK, :].rearrange("(h p) d -> p h d", h=HALVES),
+                out=out[0, first : first + len(halves) * P, :].rearrange("(h p) d -> p h d", h=len(halves)),
                 in_=result[:],
             )
+
+        BOTH = (0, 1)
+        LAST = N_BLOCKS - 1
 
         def is_block(n):
             return 0 <= n < N_BLOCKS
 
         with tc.manual_schedule():
-            transpose_rows(0)
-            transpose_rows(1)
-            copy_rows(0, nc.vector.tensor_copy)
-            copy_rows(1, nc.scalar.copy)
-            transpose_rows(2)
+            Q, K = 0, 1
+            transpose_rows(0, K, psum_b, "bank")
+            transpose_rows(0, Q, psum_b, "bank")
+            transpose_rows(BLOCK, Q, psum_t, "turned")
+            transpose_rows(BLOCK, K, psum_t, "turned")
+            copy_rows(0, K, nc.vector.tensor_copy)
+            copy_rows(0, Q, nc.scalar.copy)
+            copy_rows(BLOCK, Q, nc.scalar.copy)
+            copy_rows(BLOCK, K, nc.vector.tensor_copy)
             group_v(0)
-            for k in range(N_BLOCKS + 4):
-                if is_block(k - 4):
-                    divide_and_store(k - 4, on_vector=(k >= N_BLOCKS))
-                if is_block(k - 3):
-                    quantise_e(k - 3)
-                if is_block(k - 2):
-                    invert_row_sums(k - 2)
+
+            def flip(i):
+                if 2 <= i < 2 * N_LOADS:
+                    transpose_rows(i // 2 * ROWS, i % 2, psum_b, "bank")
+
+            def unflip(i, copy):
+                if 2 <= i < 2 * N_LOADS:
+                    copy_rows(i // 2 * ROWS, i % 2, copy)
+
+            for k in range(N_BLOCKS):
+                if k >= 2:
+                    unflip(k + 2, nc.vector.tensor_copy)
+                score(k, 0)
+                take_max(k, 0)
+                if k == 1:
+                    flip(2)
+                    unflip(2, nc.scalar.copy)
+                score(k, 1)
+                take_max(k, 1)
+                if k == 1:
+                    flip(3)
+                    unflip(3, nc.vector.tensor_copy)
+                if k < LAST:
+                    if is_block(k - 3):
+                        quantise_e(k - 3, BOTH)
+                    scale_row_max(k, BOTH)
+                    if is_block(k - 2):
+                        invert_row_sums(k - 2)
                 if k == 1:
                     quantise_v(0)
                     group_v(1)
@@ -302,18 +343,43 @@ def tile_slidingselfattention_pa_t_kernel(tc, qkv, out):
                     assemble_v(k)
                     if k // 2 + 1 < N_LOADS:
                         group_v(k // 2 + 1)
-                copy_rows(k + 2, nc.vector.tensor_copy)
-                if is_block(k):
-                    score(k, 0)
-                    score(k, 1)
-                if is_block(k - 1):
-                    exponentials(k - 1)
-                if is_block(k - 3):
-                    weighted_sum(k - 3)
-                transpose_rows(k + 3)
+                if is_block(k - 4):
+                    weighted_sum(k - 4, BOTH)
                 if is_block(k - 2):
-                    group_e(k - 2)
-                if is_block(k):
-                    scale_row_max(k)
+                    transpose_e(k - 2, BOTH)
+                if k >= 1:
+                    flip(k + 3)
                 if is_block(k - 1):
-                    transpose_e(k - 1)
+                    exponentials(k - 1, BOTH)
+                if is_block(k - 4):
+                    divide(k - 4, BOTH, on_vector=(k >= N_BLOCKS - 2))
+                if is_block(k - 2):
+                    group_e(k - 2, BOTH, nc.scalar.copy)
+            n = LAST
+            scale_row_max(n, (0,))
+            quantise_e(n - 3, BOTH)
+            scale_row_max(n, (1,))
+            invert_row_sums(n - 2)
+            transpose_e(n - 1, BOTH)
+            exponentials(n, BOTH)
+            quantise_e(n - 2, BOTH)
+            group_e(n - 1, BOTH, nc.vector.tensor_copy)
+            invert_row_sums(n - 1)
+            weighted_sum(n - 3, BOTH)
+            divide(n - 3, BOTH, True)
+            transpose_e(n, (0,))
+            weighted_sum(n - 2, BOTH)
+            transpose_e(n, (1,))
+            group_e(n, (0,), nc.scalar.copy)
+            group_e(n, (1,), nc.scalar.copy)
+            quantise_e(n - 1, BOTH)
+            invert_row_sums(n)
+            divide(n - 2, BOTH, False)
+            quantise_e(n, (0,))
+            quantise_e(n, (1,))
+            weighted_sum(n - 1, BOTH, psum_s, "s")
+            divide(n - 1, BOTH, True)
+            weighted_sum(n, (0,), psum_s, "s")
+            weighted_sum(n, (1,), psum_s, "s")
+            divide(n, (0,), False)
+            divide(n, (1,), True)

@@ -66,6 +66,8 @@ def tile_slidingselfattention_pa_t_kernel(tc, qkv, out):
             if g == 1:
                 v_rows[0] = load(0, PACK, 2 * D, 3 * D, "v_rows0")[:]
 
+        ctx.enter_context(tc.manual_schedule())
+
         ident_f32 = keep.tile([P, P], F32, name="ident_f32")
         make_identity(nc, ident_f32[:])
         ident_bf16 = keep.tile([P, P], BF16, name="ident_bf16")
@@ -296,90 +298,89 @@ def tile_slidingselfattention_pa_t_kernel(tc, qkv, out):
         def is_block(n):
             return 0 <= n < N_BLOCKS
 
-        with tc.manual_schedule():
-            Q, K = 0, 1
-            transpose_rows(0, K, psum_b, "bank")
-            transpose_rows(0, Q, psum_b, "bank")
-            transpose_rows(BLOCK, Q, psum_t, "turned")
-            transpose_rows(BLOCK, K, psum_t, "turned")
-            copy_rows(0, K, nc.vector.tensor_copy)
-            copy_rows(0, Q, nc.scalar.copy)
-            copy_rows(BLOCK, Q, nc.scalar.copy)
-            copy_rows(BLOCK, K, nc.vector.tensor_copy)
-            group_v(0)
+        Q, K = 0, 1
+        transpose_rows(0, K, psum_b, "bank")
+        transpose_rows(0, Q, psum_b, "bank")
+        transpose_rows(BLOCK, Q, psum_t, "turned")
+        transpose_rows(BLOCK, K, psum_t, "turned")
+        copy_rows(0, K, nc.vector.tensor_copy)
+        copy_rows(0, Q, nc.scalar.copy)
+        copy_rows(BLOCK, Q, nc.scalar.copy)
+        copy_rows(BLOCK, K, nc.vector.tensor_copy)
+        group_v(0)
 
-            def flip(i):
-                if 2 <= i < 2 * N_LOADS:
-                    transpose_rows(i // 2 * ROWS, i % 2, psum_b, "bank")
+        def flip(i):
+            if 2 <= i < 2 * N_LOADS:
+                transpose_rows(i // 2 * ROWS, i % 2, psum_b, "bank")
 
-            def unflip(i, copy):
-                if 2 <= i < 2 * N_LOADS:
-                    copy_rows(i // 2 * ROWS, i % 2, copy)
+        def unflip(i, copy):
+            if 2 <= i < 2 * N_LOADS:
+                copy_rows(i // 2 * ROWS, i % 2, copy)
 
-            for k in range(N_BLOCKS):
-                if k >= 2:
-                    unflip(k + 2, nc.vector.tensor_copy)
-                score(k, 0)
-                take_max(k, 0)
-                if k == 1:
-                    flip(2)
-                    unflip(2, nc.scalar.copy)
-                score(k, 1)
-                take_max(k, 1)
-                if k == 1:
-                    flip(3)
-                    unflip(3, nc.vector.tensor_copy)
-                if k < LAST:
-                    if is_block(k - 3):
-                        quantise_e(k - 3, BOTH)
-                    scale_row_max(k, BOTH)
-                    if is_block(k - 2):
-                        invert_row_sums(k - 2)
-                if k == 1:
-                    quantise_v(0)
-                    group_v(1)
-                elif k % 2 == 0 and 1 <= k // 2 < N_LOADS:
-                    quantise_v(k // 2)
-                    assemble_v(k)
-                    if k // 2 + 1 < N_LOADS:
-                        group_v(k // 2 + 1)
-                if is_block(k - 4):
-                    weighted_sum(k - 4, BOTH)
+        for k in range(N_BLOCKS):
+            if k >= 2:
+                unflip(k + 2, nc.vector.tensor_copy)
+            score(k, 0)
+            take_max(k, 0)
+            if k == 1:
+                flip(2)
+                unflip(2, nc.scalar.copy)
+            score(k, 1)
+            take_max(k, 1)
+            if k == 1:
+                flip(3)
+                unflip(3, nc.vector.tensor_copy)
+            if k < LAST:
+                if is_block(k - 3):
+                    quantise_e(k - 3, BOTH)
+                scale_row_max(k, BOTH)
                 if is_block(k - 2):
-                    transpose_e(k - 2, BOTH)
-                if k >= 1:
-                    flip(k + 3)
-                if is_block(k - 1):
-                    exponentials(k - 1, BOTH)
-                if is_block(k - 4):
-                    divide(k - 4, BOTH, on_vector=(k >= N_BLOCKS - 2))
-                if is_block(k - 2):
-                    group_e(k - 2, BOTH, nc.scalar.copy)
-            n = LAST
-            scale_row_max(n, (0,))
-            quantise_e(n - 3, BOTH)
-            scale_row_max(n, (1,))
-            invert_row_sums(n - 2)
-            transpose_e(n - 1, BOTH)
-            exponentials(n, BOTH)
-            quantise_e(n - 2, BOTH)
-            group_e(n - 1, BOTH, nc.vector.tensor_copy)
-            invert_row_sums(n - 1)
-            weighted_sum(n - 3, BOTH)
-            divide(n - 3, BOTH, True)
-            transpose_e(n, (0,))
-            weighted_sum(n - 2, BOTH)
-            transpose_e(n, (1,))
-            group_e(n, (0,), nc.scalar.copy)
-            group_e(n, (1,), nc.scalar.copy)
-            quantise_e(n - 1, BOTH)
-            invert_row_sums(n)
-            divide(n - 2, BOTH, False)
-            quantise_e(n, (0,))
-            quantise_e(n, (1,))
-            weighted_sum(n - 1, BOTH, psum_s, "s")
-            divide(n - 1, BOTH, True)
-            weighted_sum(n, (0,), psum_s, "s")
-            weighted_sum(n, (1,), psum_s, "s")
-            divide(n, (0,), False)
-            divide(n, (1,), True)
+                    invert_row_sums(k - 2)
+            if k == 1:
+                quantise_v(0)
+                group_v(1)
+            elif k % 2 == 0 and 1 <= k // 2 < N_LOADS:
+                quantise_v(k // 2)
+                assemble_v(k)
+                if k // 2 + 1 < N_LOADS:
+                    group_v(k // 2 + 1)
+            if is_block(k - 4):
+                weighted_sum(k - 4, BOTH)
+            if is_block(k - 2):
+                transpose_e(k - 2, BOTH)
+            if k >= 1:
+                flip(k + 3)
+            if is_block(k - 1):
+                exponentials(k - 1, BOTH)
+            if is_block(k - 4):
+                divide(k - 4, BOTH, on_vector=(k >= N_BLOCKS - 2))
+            if is_block(k - 2):
+                group_e(k - 2, BOTH, nc.scalar.copy)
+        n = LAST
+        scale_row_max(n, (0,))
+        quantise_e(n - 3, BOTH)
+        scale_row_max(n, (1,))
+        invert_row_sums(n - 2)
+        transpose_e(n - 1, BOTH)
+        exponentials(n, BOTH)
+        quantise_e(n - 2, BOTH)
+        group_e(n - 1, BOTH, nc.vector.tensor_copy)
+        invert_row_sums(n - 1)
+        weighted_sum(n - 3, BOTH)
+        divide(n - 3, BOTH, True)
+        transpose_e(n, (0,))
+        weighted_sum(n - 2, BOTH)
+        transpose_e(n, (1,))
+        group_e(n, (0,), nc.scalar.copy)
+        group_e(n, (1,), nc.scalar.copy)
+        quantise_e(n - 1, BOTH)
+        invert_row_sums(n)
+        divide(n - 2, BOTH, False)
+        quantise_e(n, (0,))
+        quantise_e(n, (1,))
+        weighted_sum(n - 1, BOTH, psum_s, "s")
+        divide(n - 1, BOTH, True)
+        weighted_sum(n, (0,), psum_s, "s")
+        weighted_sum(n, (1,), psum_s, "s")
+        divide(n, (0,), False)
+        divide(n, (1,), True)

@@ -32,6 +32,7 @@ SLOTS = 3
 SCALE = 1.0 / 16.0
 HIDDEN = -10000.0 / SCALE
 E_RING = 3
+WIDE = 512
 FIRST_PACK = BLOCK // P
 
 FLOPS = 2 * (2 * SEQ * WINDOW * D)
@@ -57,15 +58,27 @@ def tile_slidingselfattention_pa_t_kernel(tc, qkv, out):
             )
             return rows
 
-        qk_rows = [load(n * BLOCK, FIRST_PACK, 0, 2 * D, "first_rows%d" % n) for n in range(HALVES)]
-        raw = {}
+        first_rows = [load(n * BLOCK, FIRST_PACK, 0, 2 * D, "first_rows%d" % n) for n in range(HALVES)]
+        qk_rows = {}
         v_rows = {}
-        for g in range(1, N_LOADS):
-            raw[g] = load(g * ROWS, PACK, 0, 3 * D, "raw%d" % g)
-            v_rows[g] = raw[g][:, :, 2 * D :]
-            if g == 1:
-                v_rows[0] = load(0, PACK, 2 * D, 3 * D, "v_rows0")[:]
 
+        def load_split(g, name):
+            qk_rows[g] = load(g * ROWS, PACK, 0, 2 * D, name)[:]
+
+        def load_v(g, name):
+            v_rows[g] = load(g * ROWS, PACK, 2 * D, 3 * D, name)[:]
+
+        def load_whole(g):
+            rows = load(g * ROWS, PACK, 0, 3 * D, "rows%d" % g)
+            qk_rows[g] = rows[:, :, 0 : 2 * D]
+            v_rows[g] = rows[:, :, 2 * D :]
+
+        load_split(1, "qk_rows1")
+        load_v(0, "v_rows0")
+        load_whole(2)
+        load_v(1, "v_rows1")
+        for g in range(3, 5):
+            load_whole(g)
         ctx.enter_context(tc.manual_schedule())
 
         ident_f32 = keep.tile([P, P], F32, name="ident_f32")
@@ -82,6 +95,14 @@ def tile_slidingselfattention_pa_t_kernel(tc, qkv, out):
             out=mask[:, 1, :], in_=mask[:, 1, :], compare_op=ALU.is_ge, fill=HIDDEN,
             base=0, pattern=[[-1, CHUNK]], channel_multiplier=1,
         )
+
+        idle = keep.tile([P, WIDE], BF16, name="idle")
+        nc.vector.memset(idle[:], 0.0)
+
+        def warm_up(count):
+            for i in range(count):
+                nothing = psum_s.tile([P, WIDE], F32, name="nothing", tag="s")
+                nc.tensor.matmul(out=nothing[:], lhsT=idle[:, 0:P], rhs=idle[:], start=True, stop=True)
 
         e_first = [keep.tile([P, DUO, P, DUO], BF16, name="e_first%d" % h) for h in range(HALVES)]
         e_ring = [
@@ -110,8 +131,8 @@ def tile_slidingselfattention_pa_t_kernel(tc, qkv, out):
 
         def transpose_rows(first, which, pool, tag):
             pack = pack_of(first)
-            rows = qk_rows[first // BLOCK] if first < ROWS else raw[first // ROWS]
-            words = rows[:].bitcast(F32)
+            rows = first_rows[first // BLOCK][:] if first < ROWS else qk_rows[first // ROWS]
+            words = rows.bitcast(F32)
             flipped[first, which] = pool.tile([P, pack, P], F32, name="flipped", tag=tag)
             for j in range(pack):
                 nc.tensor.transpose(
@@ -299,6 +320,7 @@ def tile_slidingselfattention_pa_t_kernel(tc, qkv, out):
             return 0 <= n < N_BLOCKS
 
         Q, K = 0, 1
+        warm_up(4)
         transpose_rows(0, K, psum_b, "bank")
         transpose_rows(0, Q, psum_b, "bank")
         transpose_rows(BLOCK, Q, psum_t, "turned")
@@ -307,6 +329,7 @@ def tile_slidingselfattention_pa_t_kernel(tc, qkv, out):
         copy_rows(0, Q, nc.scalar.copy)
         copy_rows(BLOCK, Q, nc.scalar.copy)
         copy_rows(BLOCK, K, nc.vector.tensor_copy)
+        warm_up(1)
         group_v(0)
 
         def flip(i):
@@ -322,28 +345,28 @@ def tile_slidingselfattention_pa_t_kernel(tc, qkv, out):
                 unflip(k + 2, nc.vector.tensor_copy)
             score(k, 0)
             take_max(k, 0)
-            if k == 1:
-                flip(2)
-                unflip(2, nc.scalar.copy)
             score(k, 1)
             take_max(k, 1)
-            if k == 1:
+            if k == 0:
+                flip(2)
+                unflip(2, nc.scalar.copy)
                 flip(3)
-                unflip(3, nc.vector.tensor_copy)
+                unflip(3, nc.scalar.copy)
             if k < LAST:
                 if is_block(k - 3):
                     quantise_e(k - 3, BOTH)
                 scale_row_max(k, BOTH)
                 if is_block(k - 2):
                     invert_row_sums(k - 2)
-            if k == 1:
-                quantise_v(0)
-                group_v(1)
-            elif k % 2 == 0 and 1 <= k // 2 < N_LOADS:
-                quantise_v(k // 2)
-                assemble_v(k)
-                if k // 2 + 1 < N_LOADS:
-                    group_v(k // 2 + 1)
+            if k % 2 == 1 and k < LAST or k == LAST - 1:
+                g = k // 2
+                quantise_v(g)
+                if g >= 1:
+                    assemble_v(2 * g)
+                if g >= 1 and g + 4 < N_LOADS:
+                    load_whole(g + 4)
+                if g + 1 < N_LOADS:
+                    group_v(g + 1)
             if is_block(k - 4):
                 weighted_sum(k - 4, BOTH)
             if is_block(k - 2):
@@ -353,20 +376,21 @@ def tile_slidingselfattention_pa_t_kernel(tc, qkv, out):
             if is_block(k - 1):
                 exponentials(k - 1, BOTH)
             if is_block(k - 4):
-                divide(k - 4, BOTH, on_vector=(k >= N_BLOCKS - 2))
-            if is_block(k - 2):
+                divide(k - 4, BOTH, on_vector=False)
+            if is_block(k - 2) and k < LAST:
                 group_e(k - 2, BOTH, nc.scalar.copy)
         n = LAST
         scale_row_max(n, (0,))
         quantise_e(n - 3, BOTH)
         scale_row_max(n, (1,))
         invert_row_sums(n - 2)
+        group_e(n - 2, BOTH, nc.vector.tensor_copy)
         transpose_e(n - 1, BOTH)
         exponentials(n, BOTH)
-        quantise_e(n - 2, BOTH)
-        group_e(n - 1, BOTH, nc.vector.tensor_copy)
-        invert_row_sums(n - 1)
         weighted_sum(n - 3, BOTH)
+        invert_row_sums(n - 1)
+        quantise_e(n - 2, BOTH)
+        group_e(n - 1, BOTH, nc.scalar.copy)
         divide(n - 3, BOTH, True)
         transpose_e(n, (0,))
         weighted_sum(n - 2, BOTH)

@@ -96,13 +96,15 @@ def tile_slidingselfattention_pa_t_kernel(tc, qkv, out):
             base=0, pattern=[[-1, CHUNK]], channel_multiplier=1,
         )
 
-        idle = keep.tile([P, WIDE], BF16, name="idle")
+        idle = keep.tile([P, P], BF16, name="idle")
         nc.vector.memset(idle[:], 0.0)
 
         def warm_up(count):
+            nothing = psum_s.tile([P, WIDE], F32, name="nothing", tag="s")
             for i in range(count):
-                nothing = psum_s.tile([P, WIDE], F32, name="nothing", tag="s")
-                nc.tensor.matmul(out=nothing[:], lhsT=idle[:, 0:P], rhs=idle[:], start=True, stop=True)
+                nc.tensor.matmul(
+                    out=nothing[:], lhsT=idle[:], rhs=idle[:, 0:1].to_broadcast([P, WIDE]), start=True, stop=True
+                )
 
         e_first = [keep.tile([P, DUO, P, DUO], BF16, name="e_first%d" % h) for h in range(HALVES)]
         e_ring = [
@@ -254,8 +256,8 @@ def tile_slidingselfattention_pa_t_kernel(tc, qkv, out):
                     accum_out=row_sums[n][:, h : h + 1],
                 )
 
-        def transpose_e(n, halves):
-            flipped_e[n, halves] = psum_t.tile([P, len(halves), DUO, P], F32, name="flipped_e", tag="turned")
+        def transpose_e(n, halves, pool=psum_t, tag="turned"):
+            flipped_e[n, halves] = pool.tile([P, len(halves), DUO, P], F32, name="flipped_e", tag=tag)
             for i, h in enumerate(halves):
                 words = e_tile_of(n, h)[:].rearrange("i u p b -> i (u p b)").bitcast(F32)
                 for u in range(DUO):
@@ -320,7 +322,7 @@ def tile_slidingselfattention_pa_t_kernel(tc, qkv, out):
             return 0 <= n < N_BLOCKS
 
         Q, K = 0, 1
-        warm_up(4)
+        warm_up(5)
         transpose_rows(0, K, psum_b, "bank")
         transpose_rows(0, Q, psum_b, "bank")
         transpose_rows(BLOCK, Q, psum_t, "turned")
@@ -394,7 +396,7 @@ def tile_slidingselfattention_pa_t_kernel(tc, qkv, out):
         divide(n - 3, BOTH, True)
         transpose_e(n, (0,))
         weighted_sum(n - 2, BOTH)
-        transpose_e(n, (1,))
+        transpose_e(n, (1,), psum_s, "s")
         group_e(n, (0,), nc.scalar.copy)
         group_e(n, (1,), nc.scalar.copy)
         quantise_e(n - 1, BOTH)

@@ -30,10 +30,11 @@ N_LOADS = SEQ // ROWS
 LOAD_CHUNKS = ROWS // CHUNK
 SLOTS = 3
 SCALE = 1.0 / 16.0
-HIDDEN = -10000.0 / SCALE
+HIDDEN = -10000.0
 E_RING = 3
 WIDE = 512
-FIRST_PACK = BLOCK // P
+PAIR = 2
+FIRST_ITEMS = {0: 2, BLOCK: 2}
 
 FLOPS = 2 * (2 * SEQ * WINDOW * D)
 
@@ -58,7 +59,9 @@ def tile_slidingselfattention_pa_t_kernel(tc, qkv, out):
             )
             return rows
 
-        first_rows = [load(n * BLOCK, FIRST_PACK, 0, 2 * D, "first_rows%d" % n) for n in range(HALVES)]
+        first_rows = {
+            first: load(first, pack, 0, 2 * D, "first_rows%d" % first) for first, pack in FIRST_ITEMS.items()
+        }
         qk_rows = {}
         v_rows = {}
 
@@ -74,9 +77,10 @@ def tile_slidingselfattention_pa_t_kernel(tc, qkv, out):
             v_rows[g] = rows[:, :, 2 * D :]
 
         load_split(1, "qk_rows1")
+        load_split(2, "qk_rows2")
         load_v(0, "v_rows0")
-        load_whole(2)
         load_v(1, "v_rows1")
+        load_v(2, "v_rows2")
         for g in range(3, 5):
             load_whole(g)
         ctx.enter_context(tc.manual_schedule())
@@ -129,11 +133,11 @@ def tile_slidingselfattention_pa_t_kernel(tc, qkv, out):
         flipped = {}
 
         def pack_of(first):
-            return FIRST_PACK if first < ROWS else PACK
+            return FIRST_ITEMS.get(first, PACK)
 
         def transpose_rows(first, which, pool, tag):
             pack = pack_of(first)
-            rows = first_rows[first // BLOCK][:] if first < ROWS else qk_rows[first // ROWS]
+            rows = first_rows[first][:] if first < ROWS else qk_rows[first // ROWS]
             words = rows.bitcast(F32)
             flipped[first, which] = pool.tile([P, pack, P], F32, name="flipped", tag=tag)
             for j in range(pack):
@@ -143,10 +147,18 @@ def tile_slidingselfattention_pa_t_kernel(tc, qkv, out):
 
         def copy_rows(first, which, copy):
             pack = pack_of(first)
-            copy(
-                out=turned[which][:, first : first + pack * P].rearrange("w (p j) -> w p j", j=pack),
-                in_=flipped[first, which][:].rearrange("w j p -> w p j"),
-            )
+            target = turned[which][:, first : first + pack * P]
+            if which == 0:
+                nc.vector.tensor_scalar(
+                    out=target.bitcast(BF16).rearrange("w (p j f) -> w p j f", j=pack, f=DUO),
+                    in0=flipped[first, which][:].bitcast(BF16).rearrange("w j (p f) -> w p j f", f=DUO),
+                    scalar1=SCALE, scalar2=None, op0=ALU.mult,
+                )
+            else:
+                copy(
+                    out=target.rearrange("w (p j) -> w p j", j=pack),
+                    in_=flipped[first, which][:].rearrange("w j p -> w p j"),
+                )
 
         grouped_v = {}
 
@@ -182,7 +194,6 @@ def tile_slidingselfattention_pa_t_kernel(tc, qkv, out):
 
         scores = {}
         row_max = {}
-        shifts = {}
         row_sums = {}
         flipped_e = {}
         grouped_e = {}
@@ -225,15 +236,7 @@ def tile_slidingselfattention_pa_t_kernel(tc, qkv, out):
             nc.vector.reduce_max(
                 out=row_max[n][:, h : h + 1],
                 in_=s[:, :, first_slot(HALVES * n + h) : SLOTS, :, :].rearrange("i u k r b -> i u (k r b)"),
-                axis=AXIS.XY,
-            )
-
-        def scale_row_max(n, halves):
-            a, b = halves[0], halves[-1] + 1
-            if a == 0:
-                shifts[n] = small.tile([P, HALVES], F32, name="shift")
-            nc.vector.tensor_scalar(
-                out=shifts[n][:, a:b], in0=row_max[n][:, a:b], scalar1=-SCALE, scalar2=None, op0=ALU.mult
+                axis=AXIS.XY, negate=True,
             )
 
         def e_tile_of(n, h):
@@ -241,8 +244,8 @@ def tile_slidingselfattention_pa_t_kernel(tc, qkv, out):
 
         def exponentials(n, halves):
             for h in halves:
-                if h == 0:
-                    row_sums[n] = small.tile([P, HALVES], F32, name="row_sums")
+                if n % PAIR == 0 and h == 0:
+                    row_sums[n // PAIR] = small.tile([P, PAIR, HALVES], F32, name="row_sums")
                 u = HALVES * n + h
                 first = first_slot(u)
                 seen = SLOTS - first
@@ -252,8 +255,8 @@ def tile_slidingselfattention_pa_t_kernel(tc, qkv, out):
                         "i u p b -> i u (p b)"
                     ),
                     in_=scores[n, h][:, :, first:SLOTS, :, :].rearrange("i u k r b -> i u (k r b)"),
-                    func=ACT.Exp, bias=shifts[n][:, h : h + 1], scale=SCALE,
-                    accum_out=row_sums[n][:, h : h + 1],
+                    func=ACT.Exp, bias=row_max[n][:, h : h + 1],
+                    accum_out=row_sums[n // PAIR][:, n % PAIR, h : h + 1],
                 )
 
         def transpose_e(n, halves, pool=psum_t, tag="turned"):
@@ -292,9 +295,9 @@ def tile_slidingselfattention_pa_t_kernel(tc, qkv, out):
                     start=True, stop=True,
                 )
 
-        def invert_row_sums(n):
-            inverse[n] = small.tile([P, HALVES], F32, name="inverse")
-            nc.vector.reciprocal(out=inverse[n][:], in_=row_sums[n][:])
+        def invert_row_sums(pair):
+            inverse[pair] = small.tile([P, PAIR, HALVES], F32, name="inverse")
+            nc.vector.reciprocal(out=inverse[pair][:], in_=row_sums[pair][:])
 
         def divide(n, halves, on_vector):
             result = results.tile([P, len(halves), D], F32, name="result")
@@ -303,11 +306,11 @@ def tile_slidingselfattention_pa_t_kernel(tc, qkv, out):
                 if on_vector:
                     nc.vector.tensor_scalar(
                         out=result[:, i, :], in0=source,
-                        scalar1=inverse[n][:, h : h + 1], scalar2=None, op0=ALU.mult,
+                        scalar1=inverse[n // PAIR][:, n % PAIR, h : h + 1], scalar2=None, op0=ALU.mult,
                     )
                 else:
                     nc.scalar.activation(
-                        out=result[:, i, :], in_=source, func=ACT.Copy, scale=inverse[n][:, h : h + 1]
+                        out=result[:, i, :], in_=source, func=ACT.Copy, scale=inverse[n // PAIR][:, n % PAIR, h : h + 1]
                     )
             first = n * BLOCK + halves[0] * P
             nc.sync.dma_start(
@@ -327,10 +330,10 @@ def tile_slidingselfattention_pa_t_kernel(tc, qkv, out):
         transpose_rows(0, Q, psum_b, "bank")
         transpose_rows(BLOCK, Q, psum_t, "turned")
         transpose_rows(BLOCK, K, psum_t, "turned")
-        copy_rows(0, K, nc.vector.tensor_copy)
-        copy_rows(0, Q, nc.scalar.copy)
-        copy_rows(BLOCK, Q, nc.scalar.copy)
-        copy_rows(BLOCK, K, nc.vector.tensor_copy)
+        copy_rows(0, K, nc.scalar.copy)
+        copy_rows(0, Q, None)
+        copy_rows(BLOCK, Q, None)
+        copy_rows(BLOCK, K, nc.scalar.copy)
         warm_up(1)
         group_v(0)
 
@@ -357,11 +360,10 @@ def tile_slidingselfattention_pa_t_kernel(tc, qkv, out):
             if k < LAST:
                 if is_block(k - 3):
                     quantise_e(k - 3, BOTH)
-                scale_row_max(k, BOTH)
-                if is_block(k - 2):
-                    invert_row_sums(k - 2)
-            if k % 2 == 1 and k < LAST or k == LAST - 1:
-                g = k // 2
+                if k >= 3 and k % 2 == 1:
+                    invert_row_sums((k - 3) // 2)
+            if k == 3 or k % 2 == 0 and k >= 2:
+                g = 0 if k == 2 else k // 2
                 quantise_v(g)
                 if g >= 1:
                     assemble_v(2 * g)
@@ -378,19 +380,16 @@ def tile_slidingselfattention_pa_t_kernel(tc, qkv, out):
             if is_block(k - 1):
                 exponentials(k - 1, BOTH)
             if is_block(k - 4):
-                divide(k - 4, BOTH, on_vector=False)
+                divide(k - 4, BOTH, on_vector=(k in [13]))
             if is_block(k - 2) and k < LAST:
-                group_e(k - 2, BOTH, nc.scalar.copy)
+                group_e(k - 2, BOTH, nc.vector.tensor_copy if k in [] else nc.scalar.copy)
         n = LAST
-        scale_row_max(n, (0,))
         quantise_e(n - 3, BOTH)
-        scale_row_max(n, (1,))
-        invert_row_sums(n - 2)
+        invert_row_sums((n - 3) // 2)
         group_e(n - 2, BOTH, nc.vector.tensor_copy)
         transpose_e(n - 1, BOTH)
         exponentials(n, BOTH)
         weighted_sum(n - 3, BOTH)
-        invert_row_sums(n - 1)
         quantise_e(n - 2, BOTH)
         group_e(n - 1, BOTH, nc.scalar.copy)
         divide(n - 3, BOTH, True)
@@ -400,7 +399,7 @@ def tile_slidingselfattention_pa_t_kernel(tc, qkv, out):
         group_e(n, (0,), nc.scalar.copy)
         group_e(n, (1,), nc.scalar.copy)
         quantise_e(n - 1, BOTH)
-        invert_row_sums(n)
+        invert_row_sums(n // 2)
         divide(n - 2, BOTH, False)
         quantise_e(n, (0,))
         quantise_e(n, (1,))

@@ -33,8 +33,8 @@ SCALE = 1.0 / 16.0
 HIDDEN = -10000.0
 E_RING = 3
 WIDE = 512
+FIRST_BLOCKS = 2
 PAIR = 2
-FIRST_ITEMS = {0: 2, BLOCK: 2}
 
 FLOPS = 2 * (2 * SEQ * WINDOW * D)
 
@@ -51,38 +51,34 @@ def tile_slidingselfattention_pa_t_kernel(tc, qkv, out):
         psum_t = ctx.enter_context(tc.psum_pool(name="psum_t", bufs=2))
         psum_b = ctx.enter_context(tc.psum_pool(name="psum_b", bufs=2))
 
-        def load(first, pack, left, right, name):
-            rows = keep.tile([P, pack, right - left], BF16, name=name)
-            nc.sync.dma_start(
-                out=rows[:],
-                in_=qkv[0, first : first + pack * P, left:right].rearrange("(p j) c -> p j c", j=pack),
-            )
-            return rows
-
-        first_rows = {
-            first: load(first, pack, 0, 2 * D, "first_rows%d" % first) for first, pack in FIRST_ITEMS.items()
-        }
         qk_rows = {}
         v_rows = {}
 
-        def load_split(g, name):
-            qk_rows[g] = load(g * ROWS, PACK, 0, 2 * D, name)[:]
+        def load_qk(first, count):
+            rows = keep.tile([P, count, 2 * D], BF16, name="qk_rows%d" % first)
+            nc.sync.dma_start(
+                out=rows[:],
+                in_=qkv[0, first : first + count * P, 0 : 2 * D].rearrange("(c p) e -> p c e", c=count),
+            )
+            qk_rows[first] = rows
 
-        def load_v(g, name):
-            v_rows[g] = load(g * ROWS, PACK, 2 * D, 3 * D, name)[:]
+        def load_v(g):
+            v_rows[g] = keep.tile([P, PACK, D], BF16, name="v_rows%d" % g)
+            nc.sync.dma_start(
+                out=v_rows[g][:],
+                in_=qkv[0, g * ROWS : (g + 1) * ROWS, 2 * D : 3 * D].rearrange("(p j) c -> p j c", j=PACK),
+            )
 
-        def load_whole(g):
-            rows = load(g * ROWS, PACK, 0, 3 * D, "rows%d" % g)
-            qk_rows[g] = rows[:, :, 0 : 2 * D]
-            v_rows[g] = rows[:, :, 2 * D :]
-
-        load_split(1, "qk_rows1")
-        load_split(2, "qk_rows2")
-        load_v(0, "v_rows0")
-        load_v(1, "v_rows1")
-        load_v(2, "v_rows2")
+        for n in range(FIRST_BLOCKS):
+            load_qk(n * BLOCK, HALVES)
+        load_qk(ROWS, LOAD_CHUNKS)
+        load_qk(2 * ROWS, LOAD_CHUNKS)
+        load_v(0)
+        load_v(1)
+        load_v(2)
         for g in range(3, 5):
-            load_whole(g)
+            load_qk(g * ROWS, LOAD_CHUNKS)
+            load_v(g)
         ctx.enter_context(tc.manual_schedule())
 
         ident_f32 = keep.tile([P, P], F32, name="ident_f32")
@@ -132,40 +128,33 @@ def tile_slidingselfattention_pa_t_kernel(tc, qkv, out):
 
         flipped = {}
 
-        def pack_of(first):
-            return FIRST_ITEMS.get(first, PACK)
-
         def transpose_rows(first, which, pool, tag):
-            pack = pack_of(first)
-            rows = first_rows[first][:] if first < ROWS else qk_rows[first // ROWS]
-            words = rows.bitcast(F32)
-            flipped[first, which] = pool.tile([P, pack, P], F32, name="flipped", tag=tag)
-            for j in range(pack):
+            words = qk_rows[first][:].bitcast(F32)
+            count = words.shape[1]
+            flipped[first, which] = pool.tile([P, count * P], F32, name="flipped", tag=tag)
+            for c in range(count):
                 nc.tensor.transpose(
-                    flipped[first, which][:, j, :], words[:, j, which * PAIRS : (which + 1) * PAIRS], ident_f32[:]
+                    flipped[first, which][:, c * P : (c + 1) * P],
+                    words[:, c, which * PAIRS : (which + 1) * PAIRS],
+                    ident_f32[:],
                 )
 
         def copy_rows(first, which, copy):
-            pack = pack_of(first)
-            target = turned[which][:, first : first + pack * P]
+            source = flipped[first, which][:]
+            target = turned[which][:, first : first + source.shape[1]]
             if which == 0:
                 nc.vector.tensor_scalar(
-                    out=target.bitcast(BF16).rearrange("w (p j f) -> w p j f", j=pack, f=DUO),
-                    in0=flipped[first, which][:].bitcast(BF16).rearrange("w j (p f) -> w p j f", f=DUO),
-                    scalar1=SCALE, scalar2=None, op0=ALU.mult,
+                    out=target.bitcast(BF16), in0=source.bitcast(BF16), scalar1=SCALE, scalar2=None, op0=ALU.mult
                 )
             else:
-                copy(
-                    out=target.rearrange("w (p j) -> w p j", j=pack),
-                    in_=flipped[first, which][:].rearrange("w j p -> w p j"),
-                )
+                copy(out=target, in_=source)
 
         grouped_v = {}
 
         def group_v(g):
             grouped_v[g] = stage_v.tile([P, D, PACK], BF16, name="grouped_v", align_bytes=64)
             nc.gpsimd.tensor_scalar(
-                out=grouped_v[g][:], in0=v_rows[g].rearrange("p t d -> p d t"),
+                out=grouped_v[g][:], in0=v_rows[g][:].rearrange("p t d -> p d t"),
                 scalar1=1.0, scalar2=0.0, op0=ALU.mult, op1=ALU.add,
             )
 
@@ -368,7 +357,8 @@ def tile_slidingselfattention_pa_t_kernel(tc, qkv, out):
                 if g >= 1:
                     assemble_v(2 * g)
                 if g >= 1 and g + 4 < N_LOADS:
-                    load_whole(g + 4)
+                    load_qk((g + 4) * ROWS, LOAD_CHUNKS)
+                    load_v(g + 4)
                 if g + 1 < N_LOADS:
                     group_v(g + 1)
             if is_block(k - 4):

@@ -378,6 +378,7 @@ def tile_slidingselfattention_pa_t_kernel(tc, qkv, out):
         invert_row_sums((n - 3) // 2)
         group_e(n - 2, BOTH, nc.vector.tensor_copy)
         transpose_e(n - 1, BOTH)
+        warm_up(1)
         exponentials(n, BOTH)
         weighted_sum(n - 3, BOTH)
         quantise_e(n - 2, BOTH)
@@ -386,6 +387,7 @@ def tile_slidingselfattention_pa_t_kernel(tc, qkv, out):
         transpose_e(n, (0,))
         weighted_sum(n - 2, BOTH)
         transpose_e(n, (1,), psum_s, "s")
+        warm_up(1)
         group_e(n, (0,), nc.scalar.copy)
         group_e(n, (1,), nc.scalar.copy)
         quantise_e(n - 1, BOTH)

@@ -45,7 +45,7 @@ def tile_slidingselfattention_pa_t_kernel(tc, qkv, out):
         keep = ctx.enter_context(tc.tile_pool(name="keep", bufs=1))
         work = ctx.enter_context(tc.tile_pool(name="work", bufs=3))
         small = ctx.enter_context(tc.tile_pool(name="small", bufs=6))
-        results = ctx.enter_context(tc.tile_pool(name="results", bufs=6))
+        results = ctx.enter_context(tc.tile_pool(name="results", bufs=N_BLOCKS + 1))
         stage_v = ctx.enter_context(tc.tile_pool(name="stage_v", bufs=1))
         psum_s = ctx.enter_context(tc.psum_pool(name="psum_s", bufs=4))
         psum_t = ctx.enter_context(tc.psum_pool(name="psum_t", bufs=2))
@@ -233,7 +233,7 @@ def tile_slidingselfattention_pa_t_kernel(tc, qkv, out):
 
         def exponentials(n, halves):
             for h in halves:
-                if n % PAIR == 0 and h == 0:
+                if n // PAIR not in row_sums:
                     row_sums[n // PAIR] = small.tile([P, PAIR, HALVES], F32, name="row_sums")
                 u = HALVES * n + h
                 first = first_slot(u)
@@ -290,16 +290,16 @@ def tile_slidingselfattention_pa_t_kernel(tc, qkv, out):
 
         def divide(n, halves, on_vector):
             result = results.tile([P, len(halves), D], F32, name="result")
-            for i, h in enumerate(halves):
-                source = summed[n, halves][:, i, :]
-                if on_vector:
-                    nc.vector.tensor_scalar(
-                        out=result[:, i, :], in0=source,
-                        scalar1=inverse[n // PAIR][:, n % PAIR, h : h + 1], scalar2=None, op0=ALU.mult,
-                    )
-                else:
+            factors = inverse[n // PAIR][:, n % PAIR, halves[0] : halves[-1] + 1]
+            if on_vector:
+                nc.vector.tensor_tensor(
+                    out=result[:], in0=summed[n, halves][:],
+                    in1=factors.unsqueeze(2).to_broadcast([P, len(halves), D]), op=ALU.mult,
+                )
+            else:
+                for i in range(len(halves)):
                     nc.scalar.activation(
-                        out=result[:, i, :], in_=source, func=ACT.Copy, scale=inverse[n // PAIR][:, n % PAIR, h : h + 1]
+                        out=result[:, i, :], in_=summed[n, halves][:, i, :], func=ACT.Copy, scale=factors[:, i : i + 1]
                     )
             first = n * BLOCK + halves[0] * P
             nc.sync.dma_start(
@@ -368,7 +368,7 @@ def tile_slidingselfattention_pa_t_kernel(tc, qkv, out):
             if k >= 1:
                 flip(k + 3)
             if is_block(k - 1):
-                exponentials(k - 1, BOTH)
+                exponentials(k - 1, (1, 0))
             if is_block(k - 4):
                 divide(k - 4, BOTH, on_vector=(k in [13]))
             if is_block(k - 2) and k < LAST:

@@ -336,7 +336,7 @@ def tile_slidingselfattention_pa_t_kernel(tc, qkv, out):
 
         for k in range(N_BLOCKS):
             if k >= 2:
-                unflip(k + 2, nc.vector.tensor_copy)
+                unflip(k + 2, nc.scalar.copy if k + 2 == 7 else nc.vector.tensor_copy)
             score(k, 0)
             take_max(k, 0)
             score(k, 1)
@@ -368,7 +368,7 @@ def tile_slidingselfattention_pa_t_kernel(tc, qkv, out):
             if k >= 1:
                 flip(k + 3)
             if is_block(k - 1):
-                exponentials(k - 1, (1, 0))
+                exponentials(k - 1, BOTH)
             if is_block(k - 4):
                 divide(k - 4, BOTH, on_vector=(k in [13]))
             if is_block(k - 2) and k < LAST:

@@ -123,8 +123,13 @@ def tile_slidingselfattention_pa_t_kernel(tc, qkv, out):
             rows = turned[which][:].bitcast(BF16).rearrange("w (x f) -> w x f", f=2)
             return rows[:, first * CHUNK : (last + 1) * CHUNK, f]
 
-        v_codes = {}
-        v_scales = {}
+        v_operands = {}
+
+        def v_codes(n):
+            return v_operands[n][:, 0:D]
+
+        def v_scales(n):
+            return v_operands[n][:, D : D + D // PACK].bitcast(U8)
 
         flipped = {}
 
@@ -158,28 +163,26 @@ def tile_slidingselfattention_pa_t_kernel(tc, qkv, out):
                 scalar1=1.0, scalar2=0.0, op0=ALU.mult, op1=ALU.add,
             )
 
-        def operand_tiles(n):
-            v_codes[n] = keep.tile([P, D], U32, name="v_codes%d" % n, align_bytes=64)
-            v_scales[n] = keep.tile([P, D], U8, name="v_scales%d" % n, align_bytes=64)
+        def operand_tile(n):
+            v_operands[n] = keep.tile([P, D + D // PACK], U32, name="v_operand%d" % n, align_bytes=64)
 
         def quantise_v(g):
             n = 2 * g + 1
-            operand_tiles(n)
+            operand_tile(n)
             nc.vector.quantize_mx(
-                out=v_codes[n][:].bitcast(FP8X4),
-                scales=v_scales[n][:],
+                out=v_codes(n).bitcast(FP8X4),
+                scales=v_scales(n),
                 in_=grouped_v[g][:].rearrange("p d t -> p (d t)"),
             )
 
         def assemble_v(n):
-            operand_tiles(n)
-            for made in (v_codes, v_scales):
-                for low, source in ((0, n - 1), (P // 2, n + 1)):
-                    high = P // 2 - low
-                    nc.sync.dma_start(
-                        out=made[n][low : low + P // 2, :].bitcast(I32),
-                        in_=made[source][high : high + P // 2, :].bitcast(I32),
-                    )
+            operand_tile(n)
+            for low, source in ((0, n - 1), (P // 2, n + 1)):
+                high = P // 2 - low
+                nc.sync.dma_start(
+                    out=v_operands[n][low : low + P // 2, :].bitcast(I32),
+                    in_=v_operands[source][high : high + P // 2, :].bitcast(I32),
+                )
 
         scores = {}
         row_max = {}
@@ -279,8 +282,8 @@ def tile_slidingselfattention_pa_t_kernel(tc, qkv, out):
                     out=summed[n, halves][:, i, :],
                     lhsT=e_codes[n, halves][:, i * P : (i + 1) * P].bitcast(FP8X4),
                     lhsT_scale=e_scales[n, halves][:, i * P : (i + 1) * P],
-                    rhs=v_codes[window][:].bitcast(FP8X4),
-                    rhs_scale=v_scales[window][:],
+                    rhs=v_codes(window).bitcast(FP8X4),
+                    rhs_scale=v_scales(window),
                     start=True, stop=True,
                 )
 
@@ -334,11 +337,21 @@ def tile_slidingselfattention_pa_t_kernel(tc, qkv, out):
             if 2 <= i < 2 * N_LOADS:
                 copy_rows(i // 2 * ROWS, i % 2, copy)
 
+        def sums_of(k):
+            if k == LAST:
+                return [k - 5, k - 4]
+            return [k - 5] if k >= 5 else []
+
         for k in range(N_BLOCKS):
             if k >= 2:
                 unflip(k + 2, nc.scalar.copy if k + 2 == 7 else nc.vector.tensor_copy)
             score(k, 0)
+            if k < LAST:
+                for n in sums_of(k):
+                    weighted_sum(n, BOTH)
             take_max(k, 0)
+            if 3 <= k < LAST:
+                quantise_e(k - 3, BOTH)
             score(k, 1)
             take_max(k, 1)
             if k == 0:
@@ -346,11 +359,8 @@ def tile_slidingselfattention_pa_t_kernel(tc, qkv, out):
                 unflip(2, nc.scalar.copy)
                 flip(3)
                 unflip(3, nc.scalar.copy)
-            if k < LAST:
-                if is_block(k - 3):
-                    quantise_e(k - 3, BOTH)
-                if k >= 3 and k % 2 == 1:
-                    invert_row_sums((k - 3) // 2)
+            if 3 <= k < LAST and k % 2 == 1:
+                invert_row_sums((k - 3) // 2)
             if k == 3 or k % 2 == 0 and k >= 2:
                 g = 0 if k == 2 else k // 2
                 quantise_v(g)
@@ -361,18 +371,19 @@ def tile_slidingselfattention_pa_t_kernel(tc, qkv, out):
                     load_v(g + 4)
                 if g + 1 < N_LOADS:
                     group_v(g + 1)
-            if is_block(k - 4):
-                weighted_sum(k - 4, BOTH)
+            if k == LAST:
+                for n in sums_of(k):
+                    weighted_sum(n, BOTH)
             if is_block(k - 2):
                 transpose_e(k - 2, BOTH)
             if k >= 1:
                 flip(k + 3)
             if is_block(k - 1):
                 exponentials(k - 1, BOTH)
-            if is_block(k - 4):
-                divide(k - 4, BOTH, on_vector=(k in [13]))
+            for n in sums_of(k):
+                divide(n, BOTH, on_vector=(n == LAST - 5))
             if is_block(k - 2) and k < LAST:
-                group_e(k - 2, BOTH, nc.vector.tensor_copy if k in [] else nc.scalar.copy)
+                group_e(k - 2, BOTH, nc.scalar.copy)
         n = LAST
         quantise_e(n - 3, BOTH)
         invert_row_sums((n - 3) // 2)
@@ -389,14 +400,14 @@ def tile_slidingselfattention_pa_t_kernel(tc, qkv, out):
         transpose_e(n, (1,), psum_s, "s")
         warm_up(1)
         group_e(n, (0,), nc.scalar.copy)
-        group_e(n, (1,), nc.scalar.copy)
         quantise_e(n - 1, BOTH)
         invert_row_sums(n // 2)
         divide(n - 2, BOTH, False)
         quantise_e(n, (0,))
+        group_e(n, (1,), nc.vector.tensor_copy)
         quantise_e(n, (1,))
         weighted_sum(n - 1, BOTH, psum_s, "s")
-        divide(n - 1, BOTH, True)
+        divide(n - 1, BOTH, False)
         weighted_sum(n, (0,), psum_s, "s")
         weighted_sum(n, (1,), psum_s, "s")
         divide(n, (0,), False)

@@ -34,6 +34,8 @@ HIDDEN = -10000.0
 E_RING = 3
 WIDE = 512
 FIRST_BLOCKS = 2
+QUANTISE_STEPS = [2, 3, 5] + [2 * g for g in range(3, N_LOADS)]
+CATCH_UP = N_BLOCKS - 2
 PAIR = 2
 
 FLOPS = 2 * (2 * SEQ * WINDOW * D)
@@ -338,20 +340,28 @@ def tile_slidingselfattention_pa_t_kernel(tc, qkv, out):
                 copy_rows(i // 2 * ROWS, i % 2, copy)
 
         def sums_of(k):
-            if k == LAST:
-                return [k - 5, k - 4]
-            return [k - 5] if k >= 5 else []
+            if k < CATCH_UP:
+                return [k - 5] if k >= 5 else []
+            return [k - 5, k - 4] if k == CATCH_UP else [k - 4]
+
+        def quantise_load(g):
+            quantise_v(g)
+            if g >= 1:
+                assemble_v(2 * g)
+            if g >= 1 and g + 4 < N_LOADS:
+                load_qk((g + 4) * ROWS, LOAD_CHUNKS)
+                load_v(g + 4)
+            if g + 1 < N_LOADS:
+                group_v(g + 1)
 
         for k in range(N_BLOCKS):
             if k >= 2:
                 unflip(k + 2, nc.scalar.copy if k + 2 == 7 else nc.vector.tensor_copy)
             score(k, 0)
-            if k < LAST:
+            if k < CATCH_UP:
                 for n in sums_of(k):
                     weighted_sum(n, BOTH)
             take_max(k, 0)
-            if 3 <= k < LAST:
-                quantise_e(k - 3, BOTH)
             score(k, 1)
             take_max(k, 1)
             if k == 0:
@@ -359,19 +369,13 @@ def tile_slidingselfattention_pa_t_kernel(tc, qkv, out):
                 unflip(2, nc.scalar.copy)
                 flip(3)
                 unflip(3, nc.scalar.copy)
+            if k in QUANTISE_STEPS:
+                quantise_load(QUANTISE_STEPS.index(k))
+            if 3 <= k < LAST:
+                quantise_e(k - 3, BOTH)
             if 3 <= k < LAST and k % 2 == 1:
                 invert_row_sums((k - 3) // 2)
-            if k == 3 or k % 2 == 0 and k >= 2:
-                g = 0 if k == 2 else k // 2
-                quantise_v(g)
-                if g >= 1:
-                    assemble_v(2 * g)
-                if g >= 1 and g + 4 < N_LOADS:
-                    load_qk((g + 4) * ROWS, LOAD_CHUNKS)
-                    load_v(g + 4)
-                if g + 1 < N_LOADS:
-                    group_v(g + 1)
-            if k == LAST:
+            if k >= CATCH_UP:
                 for n in sums_of(k):
                     weighted_sum(n, BOTH)
             if is_block(k - 2):
@@ -381,7 +385,7 @@ def tile_slidingselfattention_pa_t_kernel(tc, qkv, out):
             if is_block(k - 1):
                 exponentials(k - 1, BOTH)
             for n in sums_of(k):
-                divide(n, BOTH, on_vector=(n == LAST - 5))
+                divide(n, BOTH, on_vector=(n == CATCH_UP - 4))
             if is_block(k - 2) and k < LAST:
                 group_e(k - 2, BOTH, nc.scalar.copy)
         n = LAST

from contextlib import ExitStack

import concourse.mybir as mybir
from concourse.masks import make_identity

F32 = mybir.dt.float32
BF16 = mybir.dt.bfloat16
U32 = mybir.dt.uint32
I32 = mybir.dt.int32
U8 = mybir.dt.uint8
FP8X4 = mybir.dt.float8_e4m3fn_x4
ACT = mybir.ActivationFunctionType
ALU = mybir.AluOpType
AXIS = mybir.AxisListType

P = 128
PACK = 4
SEQ = 4096
D = 256
PAIRS = D // 2
DUO = 2
BLOCK = 256
HALVES = BLOCK // P
N_BLOCKS = SEQ // BLOCK
WINDOW = 2 * BLOCK
CHUNK = 128
QUARTER = CHUNK // PACK
ROWS = P * PACK
N_LOADS = SEQ // ROWS
LOAD_CHUNKS = ROWS // CHUNK
SLOTS = 3
SCALE = 1.0 / 16.0
HIDDEN = -10000.0
E_RING = 3
WIDE = 512
FIRST_BLOCKS = 2
QUANTISE_STEPS = [2, 3, 5] + [2 * g for g in range(3, N_LOADS)]
CATCH_UP = N_BLOCKS - 2
PAIR = 2

FLOPS = 2 * (2 * SEQ * WINDOW * D)


def tile_slidingselfattention_pa_t_kernel(tc, qkv, out):
    nc = tc.nc
    with ExitStack() as ctx:
        keep = ctx.enter_context(tc.tile_pool(name="keep", bufs=1))
        work = ctx.enter_context(tc.tile_pool(name="work", bufs=3))
        small = ctx.enter_context(tc.tile_pool(name="small", bufs=6))
        results = ctx.enter_context(tc.tile_pool(name="results", bufs=N_BLOCKS + 1))
        stage_v = ctx.enter_context(tc.tile_pool(name="stage_v", bufs=1))
        psum_s = ctx.enter_context(tc.psum_pool(name="psum_s", bufs=4))
        psum_t = ctx.enter_context(tc.psum_pool(name="psum_t", bufs=2))
        psum_b = ctx.enter_context(tc.psum_pool(name="psum_b", bufs=2))

        qk_rows = {}
        v_rows = {}

        def load_qk(first, count):
            rows = keep.tile([P, count, 2 * D], BF16, name="qk_rows%d" % first)
            nc.sync.dma_start(
                out=rows[:],
                in_=qkv[0, first : first + count * P, 0 : 2 * D].rearrange("(c p) e -> p c e", c=count),
            )
            qk_rows[first] = rows

        def load_v(g):
            v_rows[g] = keep.tile([P, PACK, D], BF16, name="v_rows%d" % g)
            nc.sync.dma_start(
                out=v_rows[g][:],
                in_=qkv[0, g * ROWS : (g + 1) * ROWS, 2 * D : 3 * D].rearrange("(p j) c -> p j c", j=PACK),
            )

        for n in range(FIRST_BLOCKS):
            load_qk(n * BLOCK, HALVES)
        load_qk(ROWS, LOAD_CHUNKS)
        load_qk(2 * ROWS, LOAD_CHUNKS)
        load_v(0)
        load_v(1)
        load_v(2)
        for g in range(3, 5):
            load_qk(g * ROWS, LOAD_CHUNKS)
            load_v(g)
        ctx.enter_context(tc.manual_schedule())

        ident_f32 = keep.tile([P, P], F32, name="ident_f32")
        make_identity(nc, ident_f32[:])
        ident_bf16 = keep.tile([P, P], BF16, name="ident_bf16")
        make_identity(nc, ident_bf16[:])
        mask = keep.tile([P, 2, CHUNK], BF16, name="mask")
        nc.gpsimd.memset(mask[:], 0.0)
        nc.gpsimd.affine_select(
            out=mask[:, 0, :], in_=mask[:, 0, :], compare_op=ALU.is_ge, fill=HIDDEN,
            base=0, pattern=[[1, CHUNK]], channel_multiplier=-1,
        )
        nc.gpsimd.affine_select(
            out=mask[:, 1, :], in_=mask[:, 1, :], compare_op=ALU.is_ge, fill=HIDDEN,
            base=0, pattern=[[-1, CHUNK]], channel_multiplier=1,
        )

        idle = keep.tile([P, P], BF16, name="idle")
        nc.vector.memset(idle[:], 0.0)

        def warm_up(count):
            nothing = psum_s.tile([P, WIDE], F32, name="nothing", tag="s")
            for i in range(count):
                nc.tensor.matmul(
                    out=nothing[:], lhsT=idle[:], rhs=idle[:, 0:1].to_broadcast([P, WIDE]), start=True, stop=True
                )

        e_first = [keep.tile([P, DUO, P, DUO], BF16, name="e_first%d" % h) for h in range(HALVES)]
        e_ring = [
            [keep.tile([P, DUO, P, DUO], BF16, name="e_ring%d_%d" % (h, i)) for i in range(E_RING)]
            for h in range(HALVES)
        ]
        for h in range(HALVES):
            nc.vector.memset(e_first[h][:, :, (h + 1) * QUARTER :, :], 0.0)
            hidden = (SLOTS * (1 - h)) * QUARTER
            for e_tile in e_ring[h]:
                nc.vector.memset(e_tile[:, :, hidden : hidden + QUARTER, :], 0.0)

        turned = [keep.tile([P, SEQ], F32, name="q_t"), keep.tile([P, SEQ], F32, name="k_t")]

        def columns_of(which, first, last, f):
            rows = turned[which][:].bitcast(BF16).rearrange("w (x f) -> w x f", f=2)
            return rows[:, first * CHUNK : (last + 1) * CHUNK, f]

        v_operands = {}

        def v_codes(n):
            return v_operands[n][:, 0:D]

        def v_scales(n):
            return v_operands[n][:, D : D + D // PACK].bitcast(U8)

        flipped = {}

        def transpose_rows(first, which, pool, tag):
            words = qk_rows[first][:].bitcast(F32)
            count = words.shape[1]
            flipped[first, which] = pool.tile([P, count * P], F32, name="flipped", tag=tag)
            for c in range(count):
                nc.tensor.transpose(
                    flipped[first, which][:, c * P : (c + 1) * P],
                    words[:, c, which * PAIRS : (which + 1) * PAIRS],
                    ident_f32[:],
                )

        def copy_rows(first, which, copy):
            source = flipped[first, which][:]
            target = turned[which][:, first : first + source.shape[1]]
            if which == 0:
                nc.vector.tensor_scalar(
                    out=target.bitcast(BF16), in0=source.bitcast(BF16), scalar1=SCALE, scalar2=None, op0=ALU.mult
                )
            else:
                copy(out=target, in_=source)

        grouped_v = {}

        def group_v(g):
            grouped_v[g] = stage_v.tile([P, D, PACK], BF16, name="grouped_v", align_bytes=64)
            nc.gpsimd.tensor_scalar(
                out=grouped_v[g][:], in0=v_rows[g][:].rearrange("p t d -> p d t"),
                scalar1=1.0, scalar2=0.0, op0=ALU.mult, op1=ALU.add,
            )

        def operand_tile(n):
            v_operands[n] = keep.tile([P, D + D // PACK], U32, name="v_operand%d" % n, align_bytes=64)

        def quantise_v(g):
            n = 2 * g + 1
            operand_tile(n)
            nc.vector.quantize_mx(
                out=v_codes(n).bitcast(FP8X4),
                scales=v_scales(n),
                in_=grouped_v[g][:].rearrange("p d t -> p (d t)"),
            )

        def assemble_v(n):
            operand_tile(n)
            for low, source in ((0, n - 1), (P // 2, n + 1)):
                high = P // 2 - low
                nc.sync.dma_start(
                    out=v_operands[n][low : low + P // 2, :].bitcast(I32),
                    in_=v_operands[source][high : high + P // 2, :].bitcast(I32),
                )

        scores = {}
        row_max = {}
        row_sums = {}
        flipped_e = {}
        grouped_e = {}
        e_codes = {}
        e_scales = {}
        summed = {}
        inverse = {}

        def first_slot(u):
            return max(0, SLOTS - 1 - u)

        def score(n, h):
            u = HALVES * n + h
            s = psum_s.tile([P, DUO, SLOTS, QUARTER, DUO], F32, name="s", tag="s")
            first = first_slot(u)

            def columns(a, b):
                return s[:, :, a:b, :, :].rearrange("i u k r b -> i (k r) u b")

            nc.tensor.matmul(
                out=columns(first, SLOTS), lhsT=columns_of(0, u, u, 0), rhs=columns_of(1, u - 2 + first, u, 0),
                start=True, stop=False,
            )
            for slot in (0, 2):
                if slot >= first:
                    nc.tensor.matmul(
                        out=columns(slot, slot + 1), lhsT=ident_bf16[:], rhs=mask[:, slot // 2, :],
                        start=False, stop=False,
                    )
            nc.tensor.matmul(
                out=columns(first, SLOTS), lhsT=columns_of(0, u, u, 1), rhs=columns_of(1, u - 2 + first, u, 1),
                start=False, stop=True,
            )
            scores[n, h] = s

        def take_max(n, h):
            if h == 0:
                row_max[n] = small.tile([P, HALVES], F32, name="row_max")
            s = scores[n, h]
            nc.vector.reduce_max(
                out=row_max[n][:, h : h + 1],
                in_=s[:, :, first_slot(HALVES * n + h) : SLOTS, :, :].rearrange("i u k r b -> i u (k r b)"),
                axis=AXIS.XY, negate=True,
            )

        def e_tile_of(n, h):
            return e_first[h] if n == 0 else e_ring[h][n % E_RING]

        def exponentials(n, halves):
            for h in halves:
                if n // PAIR not in row_sums:
                    row_sums[n // PAIR] = small.tile([P, PAIR, HALVES], F32, name="row_sums")
                u = HALVES * n + h
                first = first_slot(u)
                seen = SLOTS - first
                quarter = u - 2 + first - HALVES * max(n - 1, 0)
                nc.scalar.activation(
                    out=e_tile_of(n, h)[:, :, quarter * QUARTER : (quarter + seen) * QUARTER, :].rearrange(
                        "i u p b -> i u (p b)"
                    ),
                    in_=scores[n, h][:, :, first:SLOTS, :, :].rearrange("i u k r b -> i u (k r b)"),
                    func=ACT.Exp, bias=row_max[n][:, h : h + 1],
                    accum_out=row_sums[n // PAIR][:, n % PAIR, h : h + 1],
                )

        def transpose_e(n, halves, pool=psum_t, tag="turned"):
            flipped_e[n, halves] = pool.tile([P, len(halves), DUO, P], F32, name="flipped_e", tag=tag)
            for i, h in enumerate(halves):
                words = e_tile_of(n, h)[:].rearrange("i u p b -> i (u p b)").bitcast(F32)
                for u in range(DUO):
                    nc.tensor.transpose(flipped_e[n, halves][:, i, u, :], words[:, u * P : (u + 1) * P], ident_f32[:])

        def group_e(n, halves, copy):
            grouped_e[n, halves] = work.tile([P, len(halves) * P * PACK], BF16, name="grouped_e", align_bytes=64)
            copy(
                out=grouped_e[n, halves][:].bitcast(F32).rearrange("p (h i u) -> p h i u", h=len(halves), u=DUO),
                in_=flipped_e[n, halves][:].rearrange("p h u i -> p h i u"),
            )

        def quantise_e(n, halves):
            e_codes[n, halves] = work.tile([P, len(halves) * P], U32, name="e_codes", align_bytes=64)
            e_scales[n, halves] = work.tile([P, len(halves) * P], U8, name="e_scales", align_bytes=64)
            nc.vector.quantize_mx(
                out=e_codes[n, halves][:].bitcast(FP8X4),
                scales=e_scales[n, halves][:],
                in_=grouped_e[n, halves][:],
            )

        def weighted_sum(n, halves, pool=psum_b, tag="bank"):
            window = max(n, 1)
            summed[n, halves] = pool.tile([P, len(halves), D], F32, name="summed", tag=tag)
            for i in range(len(halves)):
                nc.tensor.matmul_mx(
                    out=summed[n, halves][:, i, :],
                    lhsT=e_codes[n, halves][:, i * P : (i + 1) * P].bitcast(FP8X4),
                    lhsT_scale=e_scales[n, halves][:, i * P : (i + 1) * P],
                    rhs=v_codes(window).bitcast(FP8X4),
                    rhs_scale=v_scales(window),
                    start=True, stop=True,
                )

        def invert_row_sums(pair):
            inverse[pair] = small.tile([P, PAIR, HALVES], F32, name="inverse")
            nc.vector.reciprocal(out=inverse[pair][:], in_=row_sums[pair][:])

        def divide(n, halves, on_vector):
            result = results.tile([P, len(halves), D], F32, name="result")
            factors = inverse[n // PAIR][:, n % PAIR, halves[0] : halves[-1] + 1]
            if on_vector:
                nc.vector.tensor_tensor(
                    out=result[:], in0=summed[n, halves][:],
                    in1=factors.unsqueeze(2).to_broadcast([P, len(halves), D]), op=ALU.mult,
                )
            else:
                for i in range(len(halves)):
                    nc.scalar.activation(
                        out=result[:, i, :], in_=summed[n, halves][:, i, :], func=ACT.Copy, scale=factors[:, i : i + 1]
                    )
            first = n * BLOCK + halves[0] * P
            nc.sync.dma_start(
                out=out[0, first : first + len(halves) * P, :].rearrange("(h p) d -> p h d", h=len(halves)),
                in_=result[:],
            )

        BOTH = (0, 1)
        LAST = N_BLOCKS - 1

        def is_block(n):
            return 0 <= n < N_BLOCKS

        Q, K = 0, 1
        warm_up(5)
        transpose_rows(0, K, psum_b, "bank")
        transpose_rows(0, Q, psum_b, "bank")
        transpose_rows(BLOCK, Q, psum_t, "turned")
        transpose_rows(BLOCK, K, psum_t, "turned")
        copy_rows(0, K, nc.scalar.copy)
        copy_rows(0, Q, None)
        copy_rows(BLOCK, Q, None)
        copy_rows(BLOCK, K, nc.scalar.copy)
        warm_up(1)
        group_v(0)

        def flip(i):
            if 2 <= i < 2 * N_LOADS:
                transpose_rows(i // 2 * ROWS, i % 2, psum_b, "bank")

        def unflip(i, copy):
            if 2 <= i < 2 * N_LOADS:
                copy_rows(i // 2 * ROWS, i % 2, copy)

        def sums_of(k):
            if k < CATCH_UP:
                return [k - 5] if k >= 5 else []
            return [k - 5, k - 4] if k == CATCH_UP else [k - 4]

        def quantise_load(g):
            quantise_v(g)
            if g >= 1:
                assemble_v(2 * g)
            if g >= 1 and g + 4 < N_LOADS:
                load_qk((g + 4) * ROWS, LOAD_CHUNKS)
                load_v(g + 4)
            if g + 1 < N_LOADS:
                group_v(g + 1)

        for k in range(N_BLOCKS):
            if k >= 2:
                unflip(k + 2, nc.scalar.copy if k + 2 == 7 else nc.vector.tensor_copy)
            score(k, 0)
            if k < CATCH_UP:
                for n in sums_of(k):
                    weighted_sum(n, BOTH)
            take_max(k, 0)
            score(k, 1)
            take_max(k, 1)
            if k == 0:
                flip(2)
                unflip(2, nc.scalar.copy)
                flip(3)
                unflip(3, nc.scalar.copy)
            if k in QUANTISE_STEPS:
                quantise_load(QUANTISE_STEPS.index(k))
            if 3 <= k < LAST:
                quantise_e(k - 3, BOTH)
            if 3 <= k < LAST and k % 2 == 1:
                invert_row_sums((k - 3) // 2)
            if k >= CATCH_UP:
                for n in sums_of(k):
                    weighted_sum(n, BOTH)
            if is_block(k - 2):
                transpose_e(k - 2, BOTH)
            if k >= 1:
                flip(k + 3)
            if is_block(k - 1):
                exponentials(k - 1, BOTH)
            for n in sums_of(k):
                divide(n, BOTH, on_vector=(n == CATCH_UP - 4))
            if is_block(k - 2) and k < LAST:
                group_e(k - 2, BOTH, nc.scalar.copy)
        n = LAST
        quantise_e(n - 3, BOTH)
        invert_row_sums((n - 3) // 2)
        group_e(n - 2, BOTH, nc.vector.tensor_copy)
        transpose_e(n - 1, BOTH)
        warm_up(1)
        exponentials(n, BOTH)
        weighted_sum(n - 3, BOTH)
        quantise_e(n - 2, BOTH)
        group_e(n - 1, BOTH, nc.scalar.copy)
        divide(n - 3, BOTH, True)
        transpose_e(n, (0,))
        weighted_sum(n - 2, BOTH)
        transpose_e(n, (1,), psum_s, "s")
        warm_up(1)
        group_e(n, (0,), nc.scalar.copy)
        quantise_e(n - 1, BOTH)
        invert_row_sums(n // 2)
        divide(n - 2, BOTH, False)
        quantise_e(n, (0,))
        group_e(n, (1,), nc.vector.tensor_copy)
        quantise_e(n, (1,))
        weighted_sum(n - 1, BOTH, psum_s, "s")
        divide(n - 1, BOTH, False)
        weighted_sum(n, (0,), psum_s, "s")
        weighted_sum(n, (1,), psum_s, "s")
        divide(n, (0,), False)
        divide(n, (1,), True)
